import numpy as np
import ml_dtypes


def mxq(x, axis, fmt="e4m3"):
    dtype, down = {"e4m3": (ml_dtypes.float8_e4m3fn, 7), "e5m2": (ml_dtypes.float8_e5m2, 14)}[fmt]
    v = np.moveaxis(np.asarray(x, np.float32).astype(ml_dtypes.bfloat16).astype(np.float64), axis, -1)
    blocks = v.reshape(v.shape[:-1] + (-1, 32))
    amax = np.abs(blocks).max(-1, keepdims=True)
    byte = np.maximum(np.where(amax > 0, np.frexp(amax)[1] - 1 + 127, 0) - down, 1)
    scale = np.exp2(byte - 127.0)
    codes = (blocks / scale).astype(np.float32).astype(dtype).astype(np.float64)
    return np.moveaxis((codes * scale).reshape(v.shape), -1, axis)


WIDE = False


def mx_kscale(k):
    if not WIDE:
        return np.ones(k)
    levels = np.array([10, -10, 5, -5, 0])
    a = np.random.permutation(np.resize(levels, k // 512 * 4)).reshape(k // 512, 4)
    idx = np.arange(k)
    return np.exp2(a[idx // 512, idx % 128 // 32])


BF16 = ml_dtypes.bfloat16


def bf(x):
    return np.asarray(x, np.float32).astype(BF16)


def f64(x):
    return np.asarray(x).astype(np.float64)


B, I, H = 256, 8192, 1024
SPARSITY = 0.5
TS = 1.0


def erf(v):
    a = np.minimum(np.abs(v), 6.0)
    q = 2.0 * a * a
    term, total, n = a, a, 0
    while np.any(term > 1e-18 * total):
        n += 1
        term = term * (q / (2 * n + 1))
        total = total + term
    return np.sign(v) * total * np.exp(-a * a) * 2.0 / np.sqrt(np.pi)


def gelu(v):
    return 0.5 * v * (1.0 + erf(v / np.sqrt(2.0)))


def sigmoid(v):
    return 1.0 / (1.0 + np.exp(-v))


def setup_inputs():
    s, u = mx_kscale(H), mx_kscale(I)
    rn = np.random.standard_normal
    keep = np.random.random((H, H)) > SPARSITY
    return {"ff1": bf(gelu(rn((B, H))) * s), "x": bf(rn((B, I)) * u), "hx": bf(rn((B, H))),
            "W_ff2": bf(rn((H, H)) * 1.5 / np.sqrt(H) / s), "b_ff2": bf(rn(H) * 0.3),
            "W_ta": bf(rn((H, H)) * 1.5 / np.sqrt(H)), "b_ta": bf(rn(H) * 0.3),
            "W_tb": bf(rn((H, H)) * 1.5 / np.sqrt(H)), "b_tb": bf(rn(H) * 0.3),
            "W_in": bf(rn((H, I)) / np.sqrt(I) / u), "b_in": bf(rn(H) * 0.3), "input_b": bf(rn(H) * 0.3),
            "W_r": bf(rn((H, H)) * keep / np.sqrt((1.0 - SPARSITY) * H)), "r_b": bf(rn(H) * 0.3)}


def reference(ff1, x, hx, W_ff2, b_ff2, W_ta, b_ta, W_tb, b_tb, W_in, b_in, input_b, W_r, r_b):
    h0 = f64(hx)
    ff2 = gelu((mxq(f64(ff1), 1, "e4m3") @ mxq(f64(W_ff2), 1, "e4m3").T) + f64(b_ff2))
    ff2q = mxq(ff2, 1, "e4m3")
    t_a = (ff2q @ mxq(f64(W_ta), 1, "e4m3").T) + f64(b_ta)
    t_b = (ff2q @ mxq(f64(W_tb), 1, "e4m3").T) + f64(b_tb)
    t_interp = sigmoid(t_a * TS + t_b)
    input_contrib = gelu((mxq(f64(x), 1, "e4m3") @ mxq(f64(W_in), 1, "e4m3").T) + f64(b_in) + f64(input_b))
    recurrent_contrib = gelu((mxq(h0, 1, "e4m3") @ mxq(f64(W_r), 1, "e4m3").T) + f64(r_b))
    return h0 * (1.0 - t_interp) + t_interp * (input_contrib + recurrent_contrib)

@@ -1,0 +1,304 @@
+from contextlib import ExitStack
+
+import concourse.mybir as mybir
+from concourse.masks import make_identity
+
+F32 = mybir.dt.float32
+BF16 = mybir.dt.bfloat16
+U32 = mybir.dt.uint32
+U8 = mybir.dt.uint8
+FP8X4 = mybir.dt.float8_e4m3fn_x4
+ACT = mybir.ActivationFunctionType
+ALU = mybir.AluOpType
+
+P = 128
+B, I, H = 256, 8192, 1024
+FLOPS = 2 * B * H * (I + 4 * H)
+
+K_PASS = 512
+WORDS_PASS = K_PASS // 2
+BANK = 512
+UNIT = 4096
+UNIT_WORDS = UNIT // 4
+TILES = H // P
+BATCH_TILES = B // P
+
+RAW_BUFS = 10
+AHEAD = RAW_BUFS - 1
+
+U_FF2, U_R, U_T, U_X, U_IN = 0, 2, 4, 8, 12
+IN_UNITS = 2 * TILES
+
+
+def tile_cfccell_pa_k_kernel(
+    tc, ff1, x, hx, W_ff2, b_ff2, W_ta, b_ta, W_tb, b_tb, W_in, b_in, input_b, W_r, r_b, out
+):
+    nc = tc.nc
+    with ExitStack() as ctx:
+        ctx.enter_context(tc.manual_schedule())
+        keep = ctx.enter_context(tc.tile_pool(name="keep", bufs=1))
+        raw_pool = ctx.enter_context(tc.tile_pool(name="raw", bufs=RAW_BUFS))
+        group_pool = ctx.enter_context(tc.tile_pool(name="group", bufs=3))
+        weight_pool = ctx.enter_context(tc.tile_pool(name="weight", bufs=4))
+        work = ctx.enter_context(tc.tile_pool(name="work", bufs=2))
+        flip_pool = ctx.enter_context(tc.psum_pool(name="flip", bufs=6))
+        acc_pool = ctx.enter_context(tc.psum_pool(name="acc", bufs=2))
+
+        bias_rows = keep.tile([P, 2 * P], BF16, name="bias_rows")
+        nc.vector.memset(bias_rows[:], 0.0)
+        for v, vector in enumerate((b_ff2, r_b, b_ta, b_tb, b_in, input_b)):
+            nc.scalar.dma_start(
+                out=bias_rows[4 * v : 4 * v + 4, :], in_=vector.rearrange("(r c) -> r c", c=2 * P)
+            )
+
+        def weight_halves(w):
+            rows = w.rearrange("(a p e) k -> p a (e k)", p=P, e=2)
+            return [rows[:, 0:2, :], rows[:, 2:4, :]]
+
+        x_rows = x.rearrange("(t p) k -> p t k", p=P)
+        w_in_rows = W_in.rearrange("(a p e) k -> p a e k", p=P, e=2)
+        ta_halves, tb_halves = weight_halves(W_ta), weight_halves(W_tb)
+        sources = weight_halves(W_ff2) + weight_halves(W_r)
+        sources += [ta_halves[0], tb_halves[0], ta_halves[1], tb_halves[1]]
+        sources += [x_rows[:, :, q * UNIT // 2 : (q + 1) * UNIT // 2] for q in range(4)]
+        sources += [
+            w_in_rows[:, m // 2, m % 2 : m % 2 + 1, half * UNIT : (half + 1) * UNIT]
+            for m in range(TILES)
+            for half in range(2)
+        ]
+        raws = []
+
+        def load_unit(n):
+            if n < len(sources):
+                raw = raw_pool.tile([P, UNIT], BF16, name="raw")
+                nc.sync.dma_start(
+                    out=raw[:].rearrange("p (n w) -> p n w", n=sources[n].shape[1]), in_=sources[n]
+                )
+                raws.append(raw)
+
+        ff1_raw = keep.tile([P, BATCH_TILES * H], BF16, name="ff1_raw")
+        hx_raw = keep.tile([P, BATCH_TILES * H], BF16, name="hx_raw")
+        nc.sync.dma_start(
+            out=ff1_raw[:].rearrange("p (t k) -> p t k", t=BATCH_TILES), in_=ff1.rearrange("(t p) k -> p t k", p=P)
+        )
+        load_unit(0)
+        load_unit(1)
+        nc.sync.dma_start(
+            out=hx_raw[:].rearrange("p (t k) -> p t k", t=BATCH_TILES), in_=hx.rearrange("(t p) k -> p t k", p=P)
+        )
+        for n in range(2, AHEAD):
+            load_unit(n)
+
+        identity = keep.tile([P, P], F32, name="identity")
+        make_identity(nc, identity[:])
+        warm = keep.tile([P, 2], F32, name="warm")
+        nc.vector.memset(warm[:], 0.0)
+        nc.scalar.activation(out=warm[:, 1:2], in_=warm[:, 0:1], func=ACT.Gelu)
+
+        def transpose_and_quantise(blocks, codes, scales):
+            banks = len(blocks) // 4
+            grouped = group_pool.tile([P, UNIT], BF16, name="grouped", align_bytes=64)
+            grouped_words = grouped[:].bitcast(F32)
+            for b in range(banks):
+                flipped = flip_pool.tile([P, BANK], F32, name="flipped")
+                for s in range(4):
+                    nc.tensor.transpose(flipped[:, s * P : (s + 1) * P], blocks[4 * b + s], identity[:])
+                source = flipped[:].rearrange("p (j u r) -> p j r u", j=2, u=2)
+                target = grouped_words[:, b * BANK : (b + 1) * BANK].rearrange("p (j r u) -> p j r u", j=2, u=2)
+                if b % 4 == 3:
+                    nc.vector.tensor_copy(out=target, in_=source)
+                else:
+                    nc.scalar.copy(out=target, in_=source)
+            nc.vector.quantize_mx(out=codes.bitcast(FP8X4), scales=scales, in_=grouped[:, 0 : 2 * BANK * banks])
+            return grouped
+
+        def quantise_activations(raw, passes, codes, scales):
+            words = raw.bitcast(F32)
+            blocks = [
+                words[:, (t * passes + c) * WORDS_PASS + u * P : (t * passes + c) * WORDS_PASS + (u + 1) * P]
+                for c in range(passes)
+                for t in range(BATCH_TILES)
+                for u in range(2)
+            ]
+            return transpose_and_quantise(blocks, codes, scales)
+
+        def quantise_weights(n):
+            load_unit(n + AHEAD)
+            words = raws[n][:].bitcast(F32)
+            codes = weight_pool.tile([P, UNIT_WORDS], U32, name="w_codes", align_bytes=64)
+            scales = weight_pool.tile([P, UNIT_WORDS], U8, name="w_scales", align_bytes=64)
+            transpose_and_quantise([words[:, s * P : (s + 1) * P] for s in range(UNIT // 2 // P)], codes[:], scales[:])
+            return codes, scales
+
+        def mx_pass(acc, weights, j, moving, c, start, stop):
+            nc.tensor.matmul_mx(
+                out=acc,
+                lhsT=weights[0][:, j * P : (j + 1) * P].bitcast(FP8X4),
+                lhsT_scale=weights[1][:, j * P : (j + 1) * P],
+                rhs=moving[0][:, c * B : (c + 1) * B].bitcast(FP8X4),
+                rhs_scale=moving[1][:, c * B : (c + 1) * B],
+                start=start,
+                stop=stop,
+            )
+
+        def small_products(units, moving):
+            sums = []
+            terms = [(weights, g) for weights in units for g in range(H // K_PASS)]
+            for pair in range(2):
+                acc = acc_pool.tile([P, BANK], F32, name="acc")
+                for i in range(2):
+                    for n, (weights, g) in enumerate(terms):
+                        mx_pass(
+                            acc[:, i * B : (i + 1) * B], weights, 2 * (2 * pair + i) + g, moving, g,
+                            n == 0, n == len(terms) - 1,
+                        )
+                    sums.append(acc[:, i * B : (i + 1) * B])
+            return sums
+
+        def activation_tiles(name, passes):
+            codes = keep.tile([P, passes * B], U32, name=name + "_codes", align_bytes=64)
+            scales = keep.tile([P, passes * B], U8, name=name + "_scales", align_bytes=64)
+            return codes, scales
+
+        ff1_q = activation_tiles("ff1", H // K_PASS)
+        ff2_q = activation_tiles("ff2", H // K_PASS)
+        hx_q = activation_tiles("hx", H // K_PASS)
+        x_q = activation_tiles("x", I // K_PASS)
+
+        quantise_activations(ff1_raw[:], H // K_PASS, ff1_q[0][:], ff1_q[1][:])
+        w_ff2 = [quantise_weights(U_FF2)]
+
+        flipped_bias = flip_pool.tile([P, BANK], F32, name="flipped")
+        nc.tensor.transpose(flipped_bias[:, 0:P], bias_rows[:].bitcast(F32), identity[:])
+        bias = keep.tile([P, 6 * TILES], F32, name="bias")
+        nc.vector.tensor_copy(out=bias[:], in_=flipped_bias[:, 0 : 3 * TILES].bitcast(BF16))
+        bias_ff2, bias_r = bias[:, 0:TILES], bias[:, TILES : 2 * TILES]
+        bias_sums = keep.tile([P, 2 * TILES], F32, name="bias_sums")
+        addends = bias[:, 2 * TILES : 6 * TILES].rearrange("p (s w m) -> p s w m", s=2, w=2)
+        nc.vector.tensor_tensor(
+            out=bias_sums[:].rearrange("p (s m) -> p s m", s=2), in0=addends[:, :, 0, :], in1=addends[:, :, 1, :],
+            op=ALU.add,
+        )
+        bias_t, bias_in = bias_sums[:, 0:TILES], bias_sums[:, TILES : 2 * TILES]
+
+        def hidden_layer(g):
+            ff2_t = work.tile([P, 4 * B], BF16, name="ff2_t")
+            for i, acc in enumerate(small_products([w_ff2[g]], ff1_q)):
+                nc.scalar.activation(
+                    out=ff2_t[:, i * B : (i + 1) * B], in_=acc, func=ACT.Gelu, bias=bias_ff2[:, 4 * g + i : 4 * g + i + 1]
+                )
+            grouped = group_pool.tile([P, UNIT], BF16, name="grouped", align_bytes=64)
+            nc.vector.tensor_copy(
+                out=grouped[:, 0 : 4 * B].rearrange("p (b i) -> p b i", i=4),
+                in_=ff2_t[:].rearrange("p (i b) -> p b i", i=4),
+            )
+            nc.vector.quantize_mx(
+                out=ff2_q[0][:, g * B : (g + 1) * B].bitcast(FP8X4),
+                scales=ff2_q[1][:, g * B : (g + 1) * B],
+                in_=grouped[:, 0 : 4 * B],
+            )
+
+        w_ff2.append(quantise_weights(U_FF2 + 1))
+        hidden_layer(0)
+
+        hx_grouped = quantise_activations(hx_raw[:], H // K_PASS, hx_q[0][:], hx_q[1][:])
+        hx_t = keep.tile([P, TILES * B], BF16, name="hx_t")
+        nc.vector.tensor_copy(
+            out=hx_t[:].rearrange("p (g i b) -> p g i b", g=2, i=4),
+            in_=hx_grouped[:, 0 : TILES * B].rearrange("p (g b i) -> p g i b", g=2, i=4),
+        )
+        hidden_layer(1)
+
+        rest = keep.tile([P, TILES * B], F32, name="rest")
+
+        def recurrent_part(half, weights):
+            gelu_r = work.tile([P, 4 * B], F32, name="gelu_r")
+            for i, acc in enumerate(small_products([weights], hx_q)):
+                nc.scalar.activation(
+                    out=gelu_r[:, i * B : (i + 1) * B], in_=acc, func=ACT.Gelu,
+                    bias=bias_r[:, 4 * half + i : 4 * half + i + 1],
+                )
+            columns = slice(4 * half * B, 4 * (half + 1) * B)
+            nc.vector.tensor_tensor(out=rest[:, columns], in0=gelu_r[:], in1=hx_t[:, columns], op=ALU.subtract)
+
+        w_r0 = quantise_weights(U_R)
+        w_r1 = quantise_weights(U_R + 1)
+        recurrent_part(0, w_r0)
+
+        gate = keep.tile([P, TILES * B], F32, name="gate")
+
+        def gate_part(half, units):
+            for i, acc in enumerate(small_products(units, ff2_q)):
+                m = 4 * half + i
+                nc.scalar.activation(
+                    out=gate[:, m * B : (m + 1) * B], in_=acc, func=ACT.Sigmoid, bias=bias_t[:, m : m + 1]
+                )
+
+        w_ta0 = quantise_weights(U_T)
+        recurrent_part(1, w_r1)
+        w_tb0 = quantise_weights(U_T + 1)
+        w_ta1 = quantise_weights(U_T + 2)
+        gate_part(0, [w_ta0, w_tb0])
+        w_tb1 = quantise_weights(U_T + 3)
+
+        def quantise_x(q):
+            load_unit(U_X + q + AHEAD)
+            columns = slice(q * UNIT_WORDS, (q + 1) * UNIT_WORDS)
+            quantise_activations(raws[U_X + q][:], UNIT // 2 // K_PASS, x_q[0][:, columns], x_q[1][:, columns])
+
+        quantise_x(0)
+        gate_part(1, [w_ta1, w_tb1])
+        for q in range(1, 4):
+            quantise_x(q)
+
+        w_in = []
+        sums = {}
+        blends = {}
+
+        def input_product(n):
+            m, half = divmod(n, 2)
+            a, e = divmod(m, 2)
+            if half == 0:
+                sums[m] = acc_pool.tile([P, BANK], F32, name="acc")
+            if n % 4 == 0:
+                blends[a] = work.tile([P, 2 * B], F32, name="blend")
+            for j in range(8):
+                c = 8 * half + j
+                mx_pass(sums[m][:, 0:B], w_in[n], j, x_q, c, c == 0, c == I // K_PASS - 1)
+            if half == 1:
+                nc.scalar.activation(
+                    out=blends[a][:, e * B : (e + 1) * B], in_=sums[m][:, 0:B], func=ACT.Gelu, bias=bias_in[:, m : m + 1]
+                )
+            if n % 4 == 3:
+                columns = slice(2 * a * B, 2 * (a + 1) * B)
+                nc.vector.tensor_tensor(out=blends[a][:], in0=blends[a][:], in1=rest[:, columns], op=ALU.add)
+                nc.vector.tensor_tensor(out=blends[a][:], in0=blends[a][:], in1=gate[:, columns], op=ALU.mult)
+
+        def write_out(a):
+            flipped = flip_pool.tile([P, BANK], F32, name="flipped")
+            for t in range(BATCH_TILES):
+                for e in range(2):
+                    nc.tensor.transpose(
+                        flipped[:, (2 * t + e) * P : (2 * t + e + 1) * P],
+                        blends[a][:, e * B + t * P : e * B + (t + 1) * P],
+                        identity[:],
+                    )
+            result = work.tile([P, BATCH_TILES * 2 * P], F32, name="result")
+            nc.vector.tensor_tensor(
+                out=result[:].rearrange("b (t p e) -> b t p e", t=BATCH_TILES, e=2),
+                in0=flipped[:].rearrange("b (t e p) -> b t p e", t=BATCH_TILES, e=2),
+                in1=hx_raw[:].rearrange("b (t a p e) -> b t a p e", t=BATCH_TILES, a=4, e=2)[:, :, a, :, :],
+                op=ALU.add,
+            )
+            nc.sync.dma_start(
+                out=out.rearrange("(t b) (a f) -> b t a f", b=P, a=4)[:, :, a, :],
+                in_=result[:].rearrange("b (t f) -> b t f", t=BATCH_TILES),
+            )
+
+        for n in range(IN_UNITS + 2):
+            if n < IN_UNITS:
+                w_in.append(quantise_weights(U_IN + n))
+            if n >= 2 and (n - 2) % 4 == 3:
+                write_out((n - 2) // 4)
+            if 1 <= n <= IN_UNITS:
+                input_product(n - 1)

@@ -26,8 +26,10 @@ BATCH_TILES = B // P
 RAW_BUFS = 10
 AHEAD = RAW_BUFS - 1
 
-U_FF2, U_R, U_T, U_X, U_IN = 0, 2, 4, 8, 12
+U_FF2, U_T, U_R, U_X, U_IN = 0, 2, 6, 8, 12
 IN_UNITS = 2 * TILES
+LAG = 2
+OUT_LAG = 2
 
 
 def tile_cfccell_pa_k_kernel(
@@ -39,7 +41,7 @@ def tile_cfccell_pa_k_kernel(
         keep = ctx.enter_context(tc.tile_pool(name="keep", bufs=1))
         raw_pool = ctx.enter_context(tc.tile_pool(name="raw", bufs=RAW_BUFS))
         group_pool = ctx.enter_context(tc.tile_pool(name="group", bufs=3))
-        weight_pool = ctx.enter_context(tc.tile_pool(name="weight", bufs=4))
+        weight_pool = ctx.enter_context(tc.tile_pool(name="weight", bufs=6))
         work = ctx.enter_context(tc.tile_pool(name="work", bufs=2))
         flip_pool = ctx.enter_context(tc.psum_pool(name="flip", bufs=6))
         acc_pool = ctx.enter_context(tc.psum_pool(name="acc", bufs=2))
@@ -58,8 +60,9 @@ def tile_cfccell_pa_k_kernel(
         x_rows = x.rearrange("(t p) k -> p t k", p=P)
         w_in_rows = W_in.rearrange("(a p e) k -> p a e k", p=P, e=2)
         ta_halves, tb_halves = weight_halves(W_ta), weight_halves(W_tb)
-        sources = weight_halves(W_ff2) + weight_halves(W_r)
+        sources = weight_halves(W_ff2)
         sources += [ta_halves[0], tb_halves[0], ta_halves[1], tb_halves[1]]
+        sources += weight_halves(W_r)
         sources += [x_rows[:, :, q * UNIT // 2 : (q + 1) * UNIT // 2] for q in range(4)]
         sources += [
             w_in_rows[:, m // 2, m % 2 : m % 2 + 1, half * UNIT : (half + 1) * UNIT]
@@ -81,12 +84,12 @@ def tile_cfccell_pa_k_kernel(
         nc.sync.dma_start(
             out=ff1_raw[:].rearrange("p (t k) -> p t k", t=BATCH_TILES), in_=ff1.rearrange("(t p) k -> p t k", p=P)
         )
-        load_unit(0)
-        load_unit(1)
-        nc.sync.dma_start(
-            out=hx_raw[:].rearrange("p (t k) -> p t k", t=BATCH_TILES), in_=hx.rearrange("(t p) k -> p t k", p=P)
-        )
-        for n in range(2, AHEAD):
+        for n in range(AHEAD):
+            if n == U_R:
+                nc.sync.dma_start(
+                    out=hx_raw[:].rearrange("p (t k) -> p t k", t=BATCH_TILES),
+                    in_=hx.rearrange("(t p) k -> p t k", p=P),
+                )
             load_unit(n)
 
         identity = keep.tile([P, P], F32, name="identity")
@@ -95,7 +98,7 @@ def tile_cfccell_pa_k_kernel(
         nc.vector.memset(warm[:], 0.0)
         nc.scalar.activation(out=warm[:, 1:2], in_=warm[:, 0:1], func=ACT.Gelu)
 
-        def transpose_and_quantise(blocks, codes, scales):
+        def transpose_and_quantise(blocks, codes, scales, scalar_banks=3):
             banks = len(blocks) // 4
             grouped = group_pool.tile([P, UNIT], BF16, name="grouped", align_bytes=64)
             grouped_words = grouped[:].bitcast(F32)
@@ -105,10 +108,10 @@ def tile_cfccell_pa_k_kernel(
                     nc.tensor.transpose(flipped[:, s * P : (s + 1) * P], blocks[4 * b + s], identity[:])
                 source = flipped[:].rearrange("p (j u r) -> p j r u", j=2, u=2)
                 target = grouped_words[:, b * BANK : (b + 1) * BANK].rearrange("p (j r u) -> p j r u", j=2, u=2)
-                if b % 4 == 3:
-                    nc.vector.tensor_copy(out=target, in_=source)
-                else:
+                if b % 4 < scalar_banks:
                     nc.scalar.copy(out=target, in_=source)
+                else:
+                    nc.vector.tensor_copy(out=target, in_=source)
             nc.vector.quantize_mx(out=codes.bitcast(FP8X4), scales=scales, in_=grouped[:, 0 : 2 * BANK * banks])
             return grouped
 
@@ -122,12 +125,13 @@ def tile_cfccell_pa_k_kernel(
             ]
             return transpose_and_quantise(blocks, codes, scales)
 
-        def quantise_weights(n):
+        def quantise_weights(n, scalar_banks=3):
             load_unit(n + AHEAD)
             words = raws[n][:].bitcast(F32)
             codes = weight_pool.tile([P, UNIT_WORDS], U32, name="w_codes", align_bytes=64)
             scales = weight_pool.tile([P, UNIT_WORDS], U8, name="w_scales", align_bytes=64)
-            transpose_and_quantise([words[:, s * P : (s + 1) * P] for s in range(UNIT // 2 // P)], codes[:], scales[:])
+            blocks = [words[:, s * P : (s + 1) * P] for s in range(UNIT // 2 // P)]
+            transpose_and_quantise(blocks, codes[:], scales[:], scalar_banks)
             return codes, scales
 
         def mx_pass(acc, weights, j, moving, c, start, stop):
@@ -166,7 +170,7 @@ def tile_cfccell_pa_k_kernel(
         x_q = activation_tiles("x", I // K_PASS)
 
         quantise_activations(ff1_raw[:], H // K_PASS, ff1_q[0][:], ff1_q[1][:])
-        w_ff2 = [quantise_weights(U_FF2)]
+        w_ff2 = [quantise_weights(U_FF2, scalar_banks=2)]
 
         flipped_bias = flip_pool.tile([P, BANK], F32, name="flipped")
         nc.tensor.transpose(flipped_bias[:, 0:P], bias_rows[:].bitcast(F32), identity[:])
@@ -181,49 +185,27 @@ def tile_cfccell_pa_k_kernel(
         )
         bias_t, bias_in = bias_sums[:, 0:TILES], bias_sums[:, TILES : 2 * TILES]
 
-        def hidden_layer(g):
-            ff2_t = work.tile([P, 4 * B], BF16, name="ff2_t")
+        ff2_t = {}
+
+        def hidden_products(g):
+            ff2_t[g] = work.tile([P, 4 * B], BF16, name="ff2_t")
             for i, acc in enumerate(small_products([w_ff2[g]], ff1_q)):
                 nc.scalar.activation(
-                    out=ff2_t[:, i * B : (i + 1) * B], in_=acc, func=ACT.Gelu, bias=bias_ff2[:, 4 * g + i : 4 * g + i + 1]
+                    out=ff2_t[g][:, i * B : (i + 1) * B], in_=acc, func=ACT.Gelu,
+                    bias=bias_ff2[:, 4 * g + i : 4 * g + i + 1],
                 )
+
+        def hidden_quantise(g):
             grouped = group_pool.tile([P, UNIT], BF16, name="grouped", align_bytes=64)
             nc.vector.tensor_copy(
                 out=grouped[:, 0 : 4 * B].rearrange("p (b i) -> p b i", i=4),
-                in_=ff2_t[:].rearrange("p (i b) -> p b i", i=4),
+                in_=ff2_t[g][:].rearrange("p (i b) -> p b i", i=4),
             )
             nc.vector.quantize_mx(
                 out=ff2_q[0][:, g * B : (g + 1) * B].bitcast(FP8X4),
                 scales=ff2_q[1][:, g * B : (g + 1) * B],
                 in_=grouped[:, 0 : 4 * B],
             )
-
-        w_ff2.append(quantise_weights(U_FF2 + 1))
-        hidden_layer(0)
-
-        hx_grouped = quantise_activations(hx_raw[:], H // K_PASS, hx_q[0][:], hx_q[1][:])
-        hx_t = keep.tile([P, TILES * B], BF16, name="hx_t")
-        nc.vector.tensor_copy(
-            out=hx_t[:].rearrange("p (g i b) -> p g i b", g=2, i=4),
-            in_=hx_grouped[:, 0 : TILES * B].rearrange("p (g b i) -> p g i b", g=2, i=4),
-        )
-        hidden_layer(1)
-
-        rest = keep.tile([P, TILES * B], F32, name="rest")
-
-        def recurrent_part(half, weights):
-            gelu_r = work.tile([P, 4 * B], F32, name="gelu_r")
-            for i, acc in enumerate(small_products([weights], hx_q)):
-                nc.scalar.activation(
-                    out=gelu_r[:, i * B : (i + 1) * B], in_=acc, func=ACT.Gelu,
-                    bias=bias_r[:, 4 * half + i : 4 * half + i + 1],
-                )
-            columns = slice(4 * half * B, 4 * (half + 1) * B)
-            nc.vector.tensor_tensor(out=rest[:, columns], in0=gelu_r[:], in1=hx_t[:, columns], op=ALU.subtract)
-
-        w_r0 = quantise_weights(U_R)
-        w_r1 = quantise_weights(U_R + 1)
-        recurrent_part(0, w_r0)
 
         gate = keep.tile([P, TILES * B], F32, name="gate")
 
@@ -234,22 +216,55 @@ def tile_cfccell_pa_k_kernel(
                     out=gate[:, m * B : (m + 1) * B], in_=acc, func=ACT.Sigmoid, bias=bias_t[:, m : m + 1]
                 )
 
-        w_ta0 = quantise_weights(U_T)
-        recurrent_part(1, w_r1)
-        w_tb0 = quantise_weights(U_T + 1)
-        w_ta1 = quantise_weights(U_T + 2)
-        gate_part(0, [w_ta0, w_tb0])
-        w_tb1 = quantise_weights(U_T + 3)
+        rest = keep.tile([P, TILES * B], F32, name="rest")
+        hx_t = keep.tile([P, TILES * B], BF16, name="hx_t")
+        gelu_r = {}
+
+        def recurrent_products(half, weights):
+            gelu_r[half] = work.tile([P, 4 * B], F32, name="gelu_r")
+            for i, acc in enumerate(small_products([weights], hx_q)):
+                nc.scalar.activation(
+                    out=gelu_r[half][:, i * B : (i + 1) * B], in_=acc, func=ACT.Gelu,
+                    bias=bias_r[:, 4 * half + i : 4 * half + i + 1],
+                )
+
+        def recurrent_rest(half):
+            columns = slice(4 * half * B, 4 * (half + 1) * B)
+            nc.vector.tensor_tensor(out=rest[:, columns], in0=gelu_r[half][:], in1=hx_t[:, columns], op=ALU.subtract)
 
         def quantise_x(q):
             load_unit(U_X + q + AHEAD)
             columns = slice(q * UNIT_WORDS, (q + 1) * UNIT_WORDS)
             quantise_activations(raws[U_X + q][:], UNIT // 2 // K_PASS, x_q[0][:, columns], x_q[1][:, columns])
 
-        quantise_x(0)
+        w_ff2.append(quantise_weights(U_FF2 + 1, scalar_banks=2))
+        w_ta0 = quantise_weights(U_T)
+        hidden_products(0)
+        w_tb0 = quantise_weights(U_T + 1)
+        hidden_products(1)
+        hidden_quantise(0)
+        w_ta1 = quantise_weights(U_T + 2)
+        hidden_quantise(1)
+        w_tb1 = quantise_weights(U_T + 3)
+
+        hx_grouped = quantise_activations(hx_raw[:], H // K_PASS, hx_q[0][:], hx_q[1][:])
+        nc.vector.tensor_copy(
+            out=hx_t[:].rearrange("p (g i b) -> p g i b", g=2, i=4),
+            in_=hx_grouped[:, 0 : TILES * B].rearrange("p (g b i) -> p g i b", g=2, i=4),
+        )
+        gate_part(0, [w_ta0, w_tb0])
+        w_r0 = quantise_weights(U_R, scalar_banks=2)
         gate_part(1, [w_ta1, w_tb1])
-        for q in range(1, 4):
-            quantise_x(q)
+        w_r1 = quantise_weights(U_R + 1, scalar_banks=2)
+
+        quantise_x(0)
+        recurrent_products(0, w_r0)
+        quantise_x(1)
+        recurrent_rest(0)
+        recurrent_products(1, w_r1)
+        quantise_x(2)
+        recurrent_rest(1)
+        quantise_x(3)
 
         w_in = []
         sums = {}
@@ -295,10 +310,10 @@ def tile_cfccell_pa_k_kernel(
                 in_=result[:].rearrange("b (t f) -> b t f", t=BATCH_TILES),
             )
 
-        for n in range(IN_UNITS + 2):
+        for n in range(IN_UNITS + LAG + OUT_LAG):
             if n < IN_UNITS:
                 w_in.append(quantise_weights(U_IN + n))
-            if n >= 2 and (n - 2) % 4 == 3:
-                write_out((n - 2) // 4)
-            if 1 <= n <= IN_UNITS:
-                input_product(n - 1)
+            if n >= LAG + OUT_LAG and (n - LAG - OUT_LAG) % 4 == 3:
+                write_out((n - LAG - OUT_LAG) // 4)
+            if LAG <= n < IN_UNITS + LAG:
+                input_product(n - LAG)

@@ -26,8 +26,9 @@ BATCH_TILES = B // P
 RAW_BUFS = 10
 AHEAD = RAW_BUFS - 1
 
-U_FF2, U_T, U_R, U_X, U_IN = 0, 2, 6, 8, 12
+U_FF2, U_R, U_T, U_X, U_IN = 0, 2, 4, 8, 12
 IN_UNITS = 2 * TILES
+SMALL_SCALAR_BANKS = 2
 LAG = 2
 OUT_LAG = 2
 
@@ -60,9 +61,8 @@ def tile_cfccell_pa_k_kernel(
         x_rows = x.rearrange("(t p) k -> p t k", p=P)
         w_in_rows = W_in.rearrange("(a p e) k -> p a e k", p=P, e=2)
         ta_halves, tb_halves = weight_halves(W_ta), weight_halves(W_tb)
-        sources = weight_halves(W_ff2)
+        sources = weight_halves(W_ff2) + weight_halves(W_r)
         sources += [ta_halves[0], tb_halves[0], ta_halves[1], tb_halves[1]]
-        sources += weight_halves(W_r)
         sources += [x_rows[:, :, q * UNIT // 2 : (q + 1) * UNIT // 2] for q in range(4)]
         sources += [
             w_in_rows[:, m // 2, m % 2 : m % 2 + 1, half * UNIT : (half + 1) * UNIT]
@@ -170,7 +170,7 @@ def tile_cfccell_pa_k_kernel(
         x_q = activation_tiles("x", I // K_PASS)
 
         quantise_activations(ff1_raw[:], H // K_PASS, ff1_q[0][:], ff1_q[1][:])
-        w_ff2 = [quantise_weights(U_FF2, scalar_banks=2)]
+        w_ff2 = [quantise_weights(U_FF2, SMALL_SCALAR_BANKS)]
 
         flipped_bias = flip_pool.tile([P, BANK], F32, name="flipped")
         nc.tensor.transpose(flipped_bias[:, 0:P], bias_rows[:].bitcast(F32), identity[:])
@@ -183,7 +183,9 @@ def tile_cfccell_pa_k_kernel(
             out=bias_sums[:].rearrange("p (s m) -> p s m", s=2), in0=addends[:, :, 0, :], in1=addends[:, :, 1, :],
             op=ALU.add,
         )
-        bias_t, bias_in = bias_sums[:, 0:TILES], bias_sums[:, TILES : 2 * TILES]
+        bias_in = bias_sums[:, TILES : 2 * TILES]
+        half_bias_t = keep.tile([P, TILES], F32, name="half_bias_t")
+        nc.vector.tensor_scalar_mul(out=half_bias_t[:], in0=bias_sums[:, 0:TILES], scalar1=0.5)
 
         ff2_t = {}
 
@@ -207,13 +209,13 @@ def tile_cfccell_pa_k_kernel(
                 in_=grouped[:, 0 : 4 * B],
             )
 
-        gate = keep.tile([P, TILES * B], F32, name="gate")
+        tanh_t = keep.tile([P, TILES * B], F32, name="tanh_t")
 
         def gate_part(half, units):
             for i, acc in enumerate(small_products(units, ff2_q)):
                 m = 4 * half + i
                 nc.scalar.activation(
-                    out=gate[:, m * B : (m + 1) * B], in_=acc, func=ACT.Sigmoid, bias=bias_t[:, m : m + 1]
+                    out=tanh_t[:, m * B : (m + 1) * B], in_=acc, func=ACT.Tanh, bias=half_bias_t[:, m : m + 1], scale=0.5
                 )
 
         rest = keep.tile([P, TILES * B], F32, name="rest")
@@ -237,33 +239,31 @@ def tile_cfccell_pa_k_kernel(
             columns = slice(q * UNIT_WORDS, (q + 1) * UNIT_WORDS)
             quantise_activations(raws[U_X + q][:], UNIT // 2 // K_PASS, x_q[0][:, columns], x_q[1][:, columns])
 
-        w_ff2.append(quantise_weights(U_FF2 + 1, scalar_banks=2))
-        w_ta0 = quantise_weights(U_T)
-        hidden_products(0)
-        w_tb0 = quantise_weights(U_T + 1)
-        hidden_products(1)
-        hidden_quantise(0)
-        w_ta1 = quantise_weights(U_T + 2)
-        hidden_quantise(1)
-        w_tb1 = quantise_weights(U_T + 3)
-
+        w_ff2.append(quantise_weights(U_FF2 + 1, SMALL_SCALAR_BANKS))
         hx_grouped = quantise_activations(hx_raw[:], H // K_PASS, hx_q[0][:], hx_q[1][:])
         nc.vector.tensor_copy(
             out=hx_t[:].rearrange("p (g i b) -> p g i b", g=2, i=4),
             in_=hx_grouped[:, 0 : TILES * B].rearrange("p (g b i) -> p g i b", g=2, i=4),
         )
-        gate_part(0, [w_ta0, w_tb0])
-        w_r0 = quantise_weights(U_R, scalar_banks=2)
-        gate_part(1, [w_ta1, w_tb1])
-        w_r1 = quantise_weights(U_R + 1, scalar_banks=2)
-
-        quantise_x(0)
+        w_r0 = quantise_weights(U_R, SMALL_SCALAR_BANKS)
+        hidden_products(0)
+        w_r1 = quantise_weights(U_R + 1, SMALL_SCALAR_BANKS)
+        hidden_products(1)
+        hidden_quantise(0)
+        w_ta0 = quantise_weights(U_T, SMALL_SCALAR_BANKS)
         recurrent_products(0, w_r0)
-        quantise_x(1)
-        recurrent_rest(0)
+        hidden_quantise(1)
+        w_tb0 = quantise_weights(U_T + 1, SMALL_SCALAR_BANKS)
         recurrent_products(1, w_r1)
-        quantise_x(2)
+        recurrent_rest(0)
+        w_ta1 = quantise_weights(U_T + 2, SMALL_SCALAR_BANKS)
         recurrent_rest(1)
+        w_tb1 = quantise_weights(U_T + 3, SMALL_SCALAR_BANKS)
+        gate_part(0, [w_ta0, w_tb0])
+        quantise_x(0)
+        quantise_x(1)
+        gate_part(1, [w_ta1, w_tb1])
+        quantise_x(2)
         quantise_x(3)
 
         w_in = []
@@ -287,7 +287,9 @@ def tile_cfccell_pa_k_kernel(
             if n % 4 == 3:
                 columns = slice(2 * a * B, 2 * (a + 1) * B)
                 nc.vector.tensor_tensor(out=blends[a][:], in0=blends[a][:], in1=rest[:, columns], op=ALU.add)
-                nc.vector.tensor_tensor(out=blends[a][:], in0=blends[a][:], in1=gate[:, columns], op=ALU.mult)
+                nc.vector.scalar_tensor_tensor(
+                    out=blends[a][:], in0=tanh_t[:, columns], scalar=1.0, in1=blends[a][:], op0=ALU.add, op1=ALU.mult
+                )
 
         def write_out(a):
             flipped = flip_pool.tile([P, BANK], F32, name="flipped")
@@ -299,12 +301,15 @@ def tile_cfccell_pa_k_kernel(
                         identity[:],
                     )
             result = work.tile([P, BATCH_TILES * 2 * P], F32, name="result")
-            nc.vector.tensor_tensor(
-                out=result[:].rearrange("b (t p e) -> b t p e", t=BATCH_TILES, e=2),
-                in0=flipped[:].rearrange("b (t e p) -> b t p e", t=BATCH_TILES, e=2),
-                in1=hx_raw[:].rearrange("b (t a p e) -> b t a p e", t=BATCH_TILES, a=4, e=2)[:, :, a, :, :],
-                op=ALU.add,
-            )
+            for t in range(BATCH_TILES):
+                nc.vector.scalar_tensor_tensor(
+                    out=result[:].rearrange("b (t p e) -> b t p e", t=BATCH_TILES, e=2)[:, t, :, :],
+                    in0=flipped[:].rearrange("b (t e p) -> b t p e", t=BATCH_TILES, e=2)[:, t, :, :],
+                    scalar=0.5,
+                    in1=hx_raw[:].rearrange("b (t a p e) -> b t a p e", t=BATCH_TILES, a=4, e=2)[:, t, a, :, :],
+                    op0=ALU.mult,
+                    op1=ALU.add,
+                )
             nc.sync.dma_start(
                 out=out.rearrange("(t b) (a f) -> b t a f", b=P, a=4)[:, :, a, :],
                 in_=result[:].rearrange("b (t f) -> b t f", t=BATCH_TILES),

@@ -27,10 +27,7 @@ RAW_BUFS = 10
 AHEAD = RAW_BUFS - 1
 
 U_FF2, U_R, U_T, U_X, U_IN = 0, 2, 4, 8, 12
-IN_UNITS = 2 * TILES
-SMALL_SCALAR_BANKS = 2
-LAG = 2
-OUT_LAG = 2
+GELU_UNIT_SCALAR_BANKS = 2
 
 
 def tile_cfccell_pa_k_kernel(
@@ -98,9 +95,8 @@ def tile_cfccell_pa_k_kernel(
         nc.vector.memset(warm[:], 0.0)
         nc.scalar.activation(out=warm[:, 1:2], in_=warm[:, 0:1], func=ACT.Gelu)
 
-        def transpose_and_quantise(blocks, codes, scales, scalar_banks=3):
+        def transpose_and_quantise(blocks, grouped, codes, scales, scalar_banks=3):
             banks = len(blocks) // 4
-            grouped = group_pool.tile([P, UNIT], BF16, name="grouped", align_bytes=64)
             grouped_words = grouped[:].bitcast(F32)
             for b in range(banks):
                 flipped = flip_pool.tile([P, BANK], F32, name="flipped")
@@ -113,9 +109,8 @@ def tile_cfccell_pa_k_kernel(
                 else:
                     nc.vector.tensor_copy(out=target, in_=source)
             nc.vector.quantize_mx(out=codes.bitcast(FP8X4), scales=scales, in_=grouped[:, 0 : 2 * BANK * banks])
-            return grouped
 
-        def quantise_activations(raw, passes, codes, scales):
+        def quantise_activations(raw, passes, grouped, codes, scales):
             words = raw.bitcast(F32)
             blocks = [
                 words[:, (t * passes + c) * WORDS_PASS + u * P : (t * passes + c) * WORDS_PASS + (u + 1) * P]
@@ -123,7 +118,7 @@ def tile_cfccell_pa_k_kernel(
                 for t in range(BATCH_TILES)
                 for u in range(2)
             ]
-            return transpose_and_quantise(blocks, codes, scales)
+            transpose_and_quantise(blocks, grouped, codes, scales)
 
         def quantise_weights(n, scalar_banks=3):
             load_unit(n + AHEAD)
@@ -131,7 +126,8 @@ def tile_cfccell_pa_k_kernel(
             codes = weight_pool.tile([P, UNIT_WORDS], U32, name="w_codes", align_bytes=64)
             scales = weight_pool.tile([P, UNIT_WORDS], U8, name="w_scales", align_bytes=64)
             blocks = [words[:, s * P : (s + 1) * P] for s in range(UNIT // 2 // P)]
-            transpose_and_quantise(blocks, codes[:], scales[:], scalar_banks)
+            grouped = group_pool.tile([P, UNIT], BF16, name="grouped", align_bytes=64)
+            transpose_and_quantise(blocks, grouped, codes[:], scales[:], scalar_banks)
             return codes, scales
 
         def mx_pass(acc, weights, j, moving, c, start, stop):
@@ -169,8 +165,9 @@ def tile_cfccell_pa_k_kernel(
         hx_q = activation_tiles("hx", H // K_PASS)
         x_q = activation_tiles("x", I // K_PASS)
 
-        quantise_activations(ff1_raw[:], H // K_PASS, ff1_q[0][:], ff1_q[1][:])
-        w_ff2 = [quantise_weights(U_FF2, SMALL_SCALAR_BANKS)]
+        ff1_grouped = group_pool.tile([P, UNIT], BF16, name="grouped", align_bytes=64)
+        quantise_activations(ff1_raw[:], H // K_PASS, ff1_grouped, ff1_q[0][:], ff1_q[1][:])
+        w_ff2 = [quantise_weights(U_FF2, GELU_UNIT_SCALAR_BANKS)]
 
         flipped_bias = flip_pool.tile([P, BANK], F32, name="flipped")
         nc.tensor.transpose(flipped_bias[:, 0:P], bias_rows[:].bitcast(F32), identity[:])
@@ -219,7 +216,7 @@ def tile_cfccell_pa_k_kernel(
                 )
 
         rest = keep.tile([P, TILES * B], F32, name="rest")
-        hx_t = keep.tile([P, TILES * B], BF16, name="hx_t")
+        hx_grouped = keep.tile([P, TILES * B], BF16, name="hx_grouped", align_bytes=64)
         gelu_r = {}
 
         def recurrent_products(half, weights):
@@ -232,33 +229,35 @@ def tile_cfccell_pa_k_kernel(
 
         def recurrent_rest(half):
             columns = slice(4 * half * B, 4 * (half + 1) * B)
-            nc.vector.tensor_tensor(out=rest[:, columns], in0=gelu_r[half][:], in1=hx_t[:, columns], op=ALU.subtract)
+            nc.vector.tensor_tensor(
+                out=rest[:, columns].rearrange("p (i b) -> p i b", i=4),
+                in0=gelu_r[half][:].rearrange("p (i b) -> p i b", i=4),
+                in1=hx_grouped[:, columns].rearrange("p (b i) -> p i b", i=4),
+                op=ALU.subtract,
+            )
 
         def quantise_x(q):
             load_unit(U_X + q + AHEAD)
             columns = slice(q * UNIT_WORDS, (q + 1) * UNIT_WORDS)
-            quantise_activations(raws[U_X + q][:], UNIT // 2 // K_PASS, x_q[0][:, columns], x_q[1][:, columns])
+            grouped = group_pool.tile([P, UNIT], BF16, name="grouped", align_bytes=64)
+            quantise_activations(raws[U_X + q][:], UNIT // 2 // K_PASS, grouped, x_q[0][:, columns], x_q[1][:, columns])
 
-        w_ff2.append(quantise_weights(U_FF2 + 1, SMALL_SCALAR_BANKS))
-        hx_grouped = quantise_activations(hx_raw[:], H // K_PASS, hx_q[0][:], hx_q[1][:])
-        nc.vector.tensor_copy(
-            out=hx_t[:].rearrange("p (g i b) -> p g i b", g=2, i=4),
-            in_=hx_grouped[:, 0 : TILES * B].rearrange("p (g b i) -> p g i b", g=2, i=4),
-        )
-        w_r0 = quantise_weights(U_R, SMALL_SCALAR_BANKS)
+        w_ff2.append(quantise_weights(U_FF2 + 1, GELU_UNIT_SCALAR_BANKS))
+        quantise_activations(hx_raw[:], H // K_PASS, hx_grouped, hx_q[0][:], hx_q[1][:])
+        w_r0 = quantise_weights(U_R, GELU_UNIT_SCALAR_BANKS)
         hidden_products(0)
-        w_r1 = quantise_weights(U_R + 1, SMALL_SCALAR_BANKS)
+        w_r1 = quantise_weights(U_R + 1, GELU_UNIT_SCALAR_BANKS)
         hidden_products(1)
         hidden_quantise(0)
-        w_ta0 = quantise_weights(U_T, SMALL_SCALAR_BANKS)
+        w_ta0 = quantise_weights(U_T)
         recurrent_products(0, w_r0)
         hidden_quantise(1)
-        w_tb0 = quantise_weights(U_T + 1, SMALL_SCALAR_BANKS)
+        w_tb0 = quantise_weights(U_T + 1)
         recurrent_products(1, w_r1)
         recurrent_rest(0)
-        w_ta1 = quantise_weights(U_T + 2, SMALL_SCALAR_BANKS)
+        w_ta1 = quantise_weights(U_T + 2)
         recurrent_rest(1)
-        w_tb1 = quantise_weights(U_T + 3, SMALL_SCALAR_BANKS)
+        w_tb1 = quantise_weights(U_T + 3)
         gate_part(0, [w_ta0, w_tb0])
         quantise_x(0)
         quantise_x(1)
@@ -266,25 +265,20 @@ def tile_cfccell_pa_k_kernel(
         quantise_x(2)
         quantise_x(3)
 
-        w_in = []
-        sums = {}
+        w_in = {}
         blends = {}
 
-        def input_product(n):
-            m, half = divmod(n, 2)
+        def input_product(m):
             a, e = divmod(m, 2)
-            if half == 0:
-                sums[m] = acc_pool.tile([P, BANK], F32, name="acc")
-            if n % 4 == 0:
+            if e == 0:
                 blends[a] = work.tile([P, 2 * B], F32, name="blend")
-            for j in range(8):
-                c = 8 * half + j
-                mx_pass(sums[m][:, 0:B], w_in[n], j, x_q, c, c == 0, c == I // K_PASS - 1)
-            if half == 1:
-                nc.scalar.activation(
-                    out=blends[a][:, e * B : (e + 1) * B], in_=sums[m][:, 0:B], func=ACT.Gelu, bias=bias_in[:, m : m + 1]
-                )
-            if n % 4 == 3:
+            acc = acc_pool.tile([P, BANK], F32, name="acc")
+            for c in range(I // K_PASS):
+                mx_pass(acc[:, 0:B], w_in[m][c // 8], c % 8, x_q, c, c == 0, c == I // K_PASS - 1)
+            nc.scalar.activation(
+                out=blends[a][:, e * B : (e + 1) * B], in_=acc[:, 0:B], func=ACT.Gelu, bias=bias_in[:, m : m + 1]
+            )
+            if e == 1:
                 columns = slice(2 * a * B, 2 * (a + 1) * B)
                 nc.vector.tensor_tensor(out=blends[a][:], in0=blends[a][:], in1=rest[:, columns], op=ALU.add)
                 nc.vector.scalar_tensor_tensor(
@@ -315,10 +309,10 @@ def tile_cfccell_pa_k_kernel(
                 in_=result[:].rearrange("b (t f) -> b t f", t=BATCH_TILES),
             )
 
-        for n in range(IN_UNITS + LAG + OUT_LAG):
-            if n < IN_UNITS:
-                w_in.append(quantise_weights(U_IN + n))
-            if n >= LAG + OUT_LAG and (n - LAG - OUT_LAG) % 4 == 3:
-                write_out((n - LAG - OUT_LAG) // 4)
-            if LAG <= n < IN_UNITS + LAG:
-                input_product(n - LAG)
+        for m in range(TILES + 2):
+            if m < TILES:
+                w_in[m] = [quantise_weights(U_IN + 2 * m), quantise_weights(U_IN + 2 * m + 1)]
+            if m >= 3 and m % 2 == 1:
+                write_out((m - 3) // 2)
+            if 1 <= m <= TILES:
+                input_product(m - 1)

@@ -15,19 +15,38 @@ P = 128
 B, I, H = 256, 8192, 1024
 FLOPS = 2 * B * H * (I + 4 * H)
 
-K_PASS = 512
+PACK = 4
+K_PASS = P * PACK
 WORDS_PASS = K_PASS // 2
+H_PASSES = H // K_PASS
+I_PASSES = I // K_PASS
 BANK = 512
+BANK_FLIPS = BANK // P
 UNIT = 4096
-UNIT_WORDS = UNIT // 4
+UNIT_BANKS = UNIT // 2 // BANK
+UNIT_WORDS = UNIT // PACK
+UNIT_OPERANDS = UNIT // K_PASS
 TILES = H // P
+PAIRS = TILES // 2
+HALF = UNIT_OPERANDS // H_PASSES
+assert HALF == PACK
 BATCH_TILES = B // P
+X_UNITS = B * I // (P * UNIT)
+assert X_UNITS == 4
+BIASES = 6
 
 RAW_BUFS = 10
 AHEAD = RAW_BUFS - 1
+GROUPED_BUFS = 3
+WEIGHT_BUFS = 6
+WORK_BUFS = 2
+FLIP_BANKS = 6
+SUM_BANKS = 2
+
+SCALAR_BANKS = 3
+GELU_UNIT_SCALAR_BANKS = 2
 
 U_FF2, U_R, U_T, U_X, U_IN = 0, 2, 4, 8, 12
-GELU_UNIT_SCALAR_BANKS = 2
 
 
 def tile_cfccell_pa_k_kernel(
@@ -38,29 +57,29 @@ def tile_cfccell_pa_k_kernel(
         ctx.enter_context(tc.manual_schedule())
         keep = ctx.enter_context(tc.tile_pool(name="keep", bufs=1))
         raw_pool = ctx.enter_context(tc.tile_pool(name="raw", bufs=RAW_BUFS))
-        group_pool = ctx.enter_context(tc.tile_pool(name="group", bufs=3))
-        weight_pool = ctx.enter_context(tc.tile_pool(name="weight", bufs=6))
-        work = ctx.enter_context(tc.tile_pool(name="work", bufs=2))
-        flip_pool = ctx.enter_context(tc.psum_pool(name="flip", bufs=6))
-        acc_pool = ctx.enter_context(tc.psum_pool(name="acc", bufs=2))
+        group_pool = ctx.enter_context(tc.tile_pool(name="group", bufs=GROUPED_BUFS))
+        weight_pool = ctx.enter_context(tc.tile_pool(name="weight", bufs=WEIGHT_BUFS))
+        work = ctx.enter_context(tc.tile_pool(name="work", bufs=WORK_BUFS))
+        flip_pool = ctx.enter_context(tc.psum_pool(name="flip", bufs=FLIP_BANKS))
+        acc_pool = ctx.enter_context(tc.psum_pool(name="acc", bufs=SUM_BANKS))
 
         bias_rows = keep.tile([P, 2 * P], BF16, name="bias_rows")
         nc.vector.memset(bias_rows[:], 0.0)
         for v, vector in enumerate((b_ff2, r_b, b_ta, b_tb, b_in, input_b)):
             nc.scalar.dma_start(
-                out=bias_rows[4 * v : 4 * v + 4, :], in_=vector.rearrange("(r c) -> r c", c=2 * P)
+                out=bias_rows[PAIRS * v : PAIRS * (v + 1), :], in_=vector.rearrange("(r c) -> r c", c=2 * P)
             )
 
         def weight_halves(w):
             rows = w.rearrange("(a p e) k -> p a (e k)", p=P, e=2)
-            return [rows[:, 0:2, :], rows[:, 2:4, :]]
+            return [rows[:, 0 : PAIRS // 2, :], rows[:, PAIRS // 2 : PAIRS, :]]
 
         x_rows = x.rearrange("(t p) k -> p t k", p=P)
         w_in_rows = W_in.rearrange("(a p e) k -> p a e k", p=P, e=2)
         ta_halves, tb_halves = weight_halves(W_ta), weight_halves(W_tb)
         sources = weight_halves(W_ff2) + weight_halves(W_r)
         sources += [ta_halves[0], tb_halves[0], ta_halves[1], tb_halves[1]]
-        sources += [x_rows[:, :, q * UNIT // 2 : (q + 1) * UNIT // 2] for q in range(4)]
+        sources += [x_rows[:, :, q * UNIT // 2 : (q + 1) * UNIT // 2] for q in range(X_UNITS)]
         sources += [
             w_in_rows[:, m // 2, m % 2 : m % 2 + 1, half * UNIT : (half + 1) * UNIT]
             for m in range(TILES)
@@ -95,22 +114,23 @@ def tile_cfccell_pa_k_kernel(
         nc.vector.memset(warm[:], 0.0)
         nc.scalar.activation(out=warm[:, 1:2], in_=warm[:, 0:1], func=ACT.Gelu)
 
-        def transpose_and_quantise(blocks, grouped, codes, scales, scalar_banks=3):
-            banks = len(blocks) // 4
+        def flip(blocks, grouped, scalar_banks):
             grouped_words = grouped[:].bitcast(F32)
-            for b in range(banks):
+            for b in range(len(blocks) // BANK_FLIPS):
                 flipped = flip_pool.tile([P, BANK], F32, name="flipped")
-                for s in range(4):
-                    nc.tensor.transpose(flipped[:, s * P : (s + 1) * P], blocks[4 * b + s], identity[:])
+                for s in range(BANK_FLIPS):
+                    nc.tensor.transpose(flipped[:, s * P : (s + 1) * P], blocks[BANK_FLIPS * b + s], identity[:])
                 source = flipped[:].rearrange("p (j u r) -> p j r u", j=2, u=2)
                 target = grouped_words[:, b * BANK : (b + 1) * BANK].rearrange("p (j r u) -> p j r u", j=2, u=2)
-                if b % 4 < scalar_banks:
+                if b % UNIT_BANKS < scalar_banks:
                     nc.scalar.copy(out=target, in_=source)
                 else:
                     nc.vector.tensor_copy(out=target, in_=source)
-            nc.vector.quantize_mx(out=codes.bitcast(FP8X4), scales=scales, in_=grouped[:, 0 : 2 * BANK * banks])
 
-        def quantise_activations(raw, passes, grouped, codes, scales):
+        def quantise(grouped, codes, scales):
+            nc.vector.quantize_mx(out=codes.bitcast(FP8X4), scales=scales, in_=grouped)
+
+        def flip_activations(raw, passes, grouped):
             words = raw.bitcast(F32)
             blocks = [
                 words[:, (t * passes + c) * WORDS_PASS + u * P : (t * passes + c) * WORDS_PASS + (u + 1) * P]
@@ -118,17 +138,25 @@ def tile_cfccell_pa_k_kernel(
                 for t in range(BATCH_TILES)
                 for u in range(2)
             ]
-            transpose_and_quantise(blocks, grouped, codes, scales)
+            flip(blocks, grouped, SCALAR_BANKS)
 
-        def quantise_weights(n, scalar_banks=3):
+        def flip_weights(n, scalar_banks):
             load_unit(n + AHEAD)
             words = raws[n][:].bitcast(F32)
+            grouped = group_pool.tile([P, UNIT], BF16, name="grouped", align_bytes=64)
+            flip([words[:, s * P : (s + 1) * P] for s in range(UNIT // 2 // P)], grouped, scalar_banks)
+            return grouped
+
+        def quantise_weights(grouped):
             codes = weight_pool.tile([P, UNIT_WORDS], U32, name="w_codes", align_bytes=64)
             scales = weight_pool.tile([P, UNIT_WORDS], U8, name="w_scales", align_bytes=64)
-            blocks = [words[:, s * P : (s + 1) * P] for s in range(UNIT // 2 // P)]
-            grouped = group_pool.tile([P, UNIT], BF16, name="grouped", align_bytes=64)
-            transpose_and_quantise(blocks, grouped, codes[:], scales[:], scalar_banks)
+            quantise(grouped[:], codes[:], scales[:])
             return codes, scales
+
+        def weight_pair(n, scalar_banks=SCALAR_BANKS):
+            first = flip_weights(n, scalar_banks)
+            second = flip_weights(n + 1, scalar_banks)
+            return [quantise_weights(first), quantise_weights(second)]
 
         def mx_pass(acc, weights, j, moving, c, start, stop):
             nc.tensor.matmul_mx(
@@ -143,13 +171,13 @@ def tile_cfccell_pa_k_kernel(
 
         def small_products(units, moving):
             sums = []
-            terms = [(weights, g) for weights in units for g in range(H // K_PASS)]
-            for pair in range(2):
+            terms = [(weights, g) for weights in units for g in range(H_PASSES)]
+            for pair in range(HALF // 2):
                 acc = acc_pool.tile([P, BANK], F32, name="acc")
                 for i in range(2):
                     for n, (weights, g) in enumerate(terms):
                         mx_pass(
-                            acc[:, i * B : (i + 1) * B], weights, 2 * (2 * pair + i) + g, moving, g,
+                            acc[:, i * B : (i + 1) * B], weights, H_PASSES * (2 * pair + i) + g, moving, g,
                             n == 0, n == len(terms) - 1,
                         )
                     sums.append(acc[:, i * B : (i + 1) * B])
@@ -160,22 +188,83 @@ def tile_cfccell_pa_k_kernel(
             scales = keep.tile([P, passes * B], U8, name=name + "_scales", align_bytes=64)
             return codes, scales
 
-        ff1_q = activation_tiles("ff1", H // K_PASS)
-        ff2_q = activation_tiles("ff2", H // K_PASS)
-        hx_q = activation_tiles("hx", H // K_PASS)
-        x_q = activation_tiles("x", I // K_PASS)
+        ff1_q = activation_tiles("ff1", H_PASSES)
+        ff2_q = activation_tiles("ff2", H_PASSES)
+        hx_q = activation_tiles("hx", H_PASSES)
+        x_q = activation_tiles("x", I_PASSES)
+
+        w_ff2 = []
+        ff2_t = {}
+
+        def hidden_products(g):
+            ff2_t[g] = work.tile([P, HALF * B], BF16, name="ff2_t")
+            for i, acc in enumerate(small_products([w_ff2[g]], ff1_q)):
+                nc.scalar.activation(
+                    out=ff2_t[g][:, i * B : (i + 1) * B], in_=acc, func=ACT.Gelu,
+                    bias=bias_ff2[:, HALF * g + i : HALF * g + i + 1],
+                )
+
+        def hidden_quantise(g):
+            grouped = group_pool.tile([P, UNIT], BF16, name="grouped", align_bytes=64)
+            nc.vector.tensor_copy(
+                out=grouped[:, 0 : PACK * B].rearrange("p (b i) -> p b i", i=PACK),
+                in_=ff2_t[g][:].rearrange("p (i b) -> p b i", i=HALF),
+            )
+            quantise(grouped[:, 0 : PACK * B], ff2_q[0][:, g * B : (g + 1) * B], ff2_q[1][:, g * B : (g + 1) * B])
+
+        tanh_t = keep.tile([P, TILES * B], F32, name="tanh_t")
+
+        def gate_part(half, units):
+            for i, acc in enumerate(small_products(units, ff2_q)):
+                m = HALF * half + i
+                nc.scalar.activation(
+                    out=tanh_t[:, m * B : (m + 1) * B], in_=acc, func=ACT.Tanh, bias=half_bias_t[:, m : m + 1], scale=0.5
+                )
+
+        hx_grouped = keep.tile([P, TILES * B], BF16, name="hx_grouped", align_bytes=64)
+        rest = keep.tile([P, TILES * B], F32, name="rest")
+        gelu_r = {}
+
+        def recurrent_products(half, weights):
+            gelu_r[half] = work.tile([P, HALF * B], F32, name="gelu_r")
+            for i, acc in enumerate(small_products([weights], hx_q)):
+                nc.scalar.activation(
+                    out=gelu_r[half][:, i * B : (i + 1) * B], in_=acc, func=ACT.Gelu,
+                    bias=bias_r[:, HALF * half + i : HALF * half + i + 1],
+                )
+
+        def recurrent_rest(half):
+            columns = slice(HALF * half * B, HALF * (half + 1) * B)
+            nc.vector.tensor_tensor(
+                out=rest[:, columns].rearrange("p (i b) -> p i b", i=HALF),
+                in0=gelu_r[half][:].rearrange("p (i b) -> p i b", i=HALF),
+                in1=hx_grouped[:, columns].rearrange("p (b i) -> p i b", i=PACK),
+                op=ALU.subtract,
+            )
+
+        def x_pair(q):
+            grouped = []
+            for n in (q, q + 1):
+                load_unit(U_X + n + AHEAD)
+                grouped.append(group_pool.tile([P, UNIT], BF16, name="grouped", align_bytes=64))
+                flip_activations(raws[U_X + n][:], UNIT // 2 // K_PASS, grouped[-1])
+            for i, n in enumerate((q, q + 1)):
+                columns = slice(n * UNIT_WORDS, (n + 1) * UNIT_WORDS)
+                quantise(grouped[i][:], x_q[0][:, columns], x_q[1][:, columns])
 
         ff1_grouped = group_pool.tile([P, UNIT], BF16, name="grouped", align_bytes=64)
-        quantise_activations(ff1_raw[:], H // K_PASS, ff1_grouped, ff1_q[0][:], ff1_q[1][:])
-        w_ff2 = [quantise_weights(U_FF2, GELU_UNIT_SCALAR_BANKS)]
+        flip_activations(ff1_raw[:], H_PASSES, ff1_grouped)
+        w_ff2_grouped = flip_weights(U_FF2, GELU_UNIT_SCALAR_BANKS)
+        quantise(ff1_grouped[:, 0 : BATCH_TILES * H], ff1_q[0][:], ff1_q[1][:])
+        w_ff2.append(quantise_weights(w_ff2_grouped))
 
         flipped_bias = flip_pool.tile([P, BANK], F32, name="flipped")
         nc.tensor.transpose(flipped_bias[:, 0:P], bias_rows[:].bitcast(F32), identity[:])
-        bias = keep.tile([P, 6 * TILES], F32, name="bias")
-        nc.vector.tensor_copy(out=bias[:], in_=flipped_bias[:, 0 : 3 * TILES].bitcast(BF16))
+        bias = keep.tile([P, BIASES * TILES], F32, name="bias")
+        nc.vector.tensor_copy(out=bias[:], in_=flipped_bias[:, 0 : BIASES * PAIRS].bitcast(BF16))
         bias_ff2, bias_r = bias[:, 0:TILES], bias[:, TILES : 2 * TILES]
         bias_sums = keep.tile([P, 2 * TILES], F32, name="bias_sums")
-        addends = bias[:, 2 * TILES : 6 * TILES].rearrange("p (s w m) -> p s w m", s=2, w=2)
+        addends = bias[:, 2 * TILES : BIASES * TILES].rearrange("p (s w m) -> p s w m", s=2, w=2)
         nc.vector.tensor_tensor(
             out=bias_sums[:].rearrange("p (s m) -> p s m", s=2), in0=addends[:, :, 0, :], in1=addends[:, :, 1, :],
             op=ALU.add,
@@ -184,86 +273,25 @@ def tile_cfccell_pa_k_kernel(
         half_bias_t = keep.tile([P, TILES], F32, name="half_bias_t")
         nc.vector.tensor_scalar_mul(out=half_bias_t[:], in0=bias_sums[:, 0:TILES], scalar1=0.5)
 
-        ff2_t = {}
-
-        def hidden_products(g):
-            ff2_t[g] = work.tile([P, 4 * B], BF16, name="ff2_t")
-            for i, acc in enumerate(small_products([w_ff2[g]], ff1_q)):
-                nc.scalar.activation(
-                    out=ff2_t[g][:, i * B : (i + 1) * B], in_=acc, func=ACT.Gelu,
-                    bias=bias_ff2[:, 4 * g + i : 4 * g + i + 1],
-                )
-
-        def hidden_quantise(g):
-            grouped = group_pool.tile([P, UNIT], BF16, name="grouped", align_bytes=64)
-            nc.vector.tensor_copy(
-                out=grouped[:, 0 : 4 * B].rearrange("p (b i) -> p b i", i=4),
-                in_=ff2_t[g][:].rearrange("p (i b) -> p b i", i=4),
-            )
-            nc.vector.quantize_mx(
-                out=ff2_q[0][:, g * B : (g + 1) * B].bitcast(FP8X4),
-                scales=ff2_q[1][:, g * B : (g + 1) * B],
-                in_=grouped[:, 0 : 4 * B],
-            )
-
-        tanh_t = keep.tile([P, TILES * B], F32, name="tanh_t")
-
-        def gate_part(half, units):
-            for i, acc in enumerate(small_products(units, ff2_q)):
-                m = 4 * half + i
-                nc.scalar.activation(
-                    out=tanh_t[:, m * B : (m + 1) * B], in_=acc, func=ACT.Tanh, bias=half_bias_t[:, m : m + 1], scale=0.5
-                )
-
-        rest = keep.tile([P, TILES * B], F32, name="rest")
-        hx_grouped = keep.tile([P, TILES * B], BF16, name="hx_grouped", align_bytes=64)
-        gelu_r = {}
-
-        def recurrent_products(half, weights):
-            gelu_r[half] = work.tile([P, 4 * B], F32, name="gelu_r")
-            for i, acc in enumerate(small_products([weights], hx_q)):
-                nc.scalar.activation(
-                    out=gelu_r[half][:, i * B : (i + 1) * B], in_=acc, func=ACT.Gelu,
-                    bias=bias_r[:, 4 * half + i : 4 * half + i + 1],
-                )
-
-        def recurrent_rest(half):
-            columns = slice(4 * half * B, 4 * (half + 1) * B)
-            nc.vector.tensor_tensor(
-                out=rest[:, columns].rearrange("p (i b) -> p i b", i=4),
-                in0=gelu_r[half][:].rearrange("p (i b) -> p i b", i=4),
-                in1=hx_grouped[:, columns].rearrange("p (b i) -> p i b", i=4),
-                op=ALU.subtract,
-            )
-
-        def quantise_x(q):
-            load_unit(U_X + q + AHEAD)
-            columns = slice(q * UNIT_WORDS, (q + 1) * UNIT_WORDS)
-            grouped = group_pool.tile([P, UNIT], BF16, name="grouped", align_bytes=64)
-            quantise_activations(raws[U_X + q][:], UNIT // 2 // K_PASS, grouped, x_q[0][:, columns], x_q[1][:, columns])
-
-        w_ff2.append(quantise_weights(U_FF2 + 1, GELU_UNIT_SCALAR_BANKS))
-        quantise_activations(hx_raw[:], H // K_PASS, hx_grouped, hx_q[0][:], hx_q[1][:])
-        w_r0 = quantise_weights(U_R, GELU_UNIT_SCALAR_BANKS)
+        w_ff2_grouped = flip_weights(U_FF2 + 1, GELU_UNIT_SCALAR_BANKS)
+        flip_activations(hx_raw[:], H_PASSES, hx_grouped)
+        w_ff2.append(quantise_weights(w_ff2_grouped))
+        quantise(hx_grouped[:], hx_q[0][:], hx_q[1][:])
         hidden_products(0)
-        w_r1 = quantise_weights(U_R + 1, GELU_UNIT_SCALAR_BANKS)
+        w_r = weight_pair(U_R, GELU_UNIT_SCALAR_BANKS)
         hidden_products(1)
         hidden_quantise(0)
-        w_ta0 = quantise_weights(U_T)
-        recurrent_products(0, w_r0)
+        w_t0 = weight_pair(U_T)
         hidden_quantise(1)
-        w_tb0 = quantise_weights(U_T + 1)
-        recurrent_products(1, w_r1)
+        recurrent_products(0, w_r[0])
+        recurrent_products(1, w_r[1])
+        w_t1 = weight_pair(U_T + 2)
         recurrent_rest(0)
-        w_ta1 = quantise_weights(U_T + 2)
         recurrent_rest(1)
-        w_tb1 = quantise_weights(U_T + 3)
-        gate_part(0, [w_ta0, w_tb0])
-        quantise_x(0)
-        quantise_x(1)
-        gate_part(1, [w_ta1, w_tb1])
-        quantise_x(2)
-        quantise_x(3)
+        gate_part(0, w_t0)
+        x_pair(0)
+        gate_part(1, w_t1)
+        x_pair(2)
 
         w_in = {}
         blends = {}
@@ -272,18 +300,16 @@ def tile_cfccell_pa_k_kernel(
             a, e = divmod(m, 2)
             if e == 0:
                 blends[a] = work.tile([P, 2 * B], F32, name="blend")
+            blend = blends[a][:, e * B : (e + 1) * B]
             acc = acc_pool.tile([P, BANK], F32, name="acc")
-            for c in range(I // K_PASS):
-                mx_pass(acc[:, 0:B], w_in[m][c // 8], c % 8, x_q, c, c == 0, c == I // K_PASS - 1)
-            nc.scalar.activation(
-                out=blends[a][:, e * B : (e + 1) * B], in_=acc[:, 0:B], func=ACT.Gelu, bias=bias_in[:, m : m + 1]
+            for c in range(I_PASSES):
+                mx_pass(acc[:, 0:B], w_in[m][c // UNIT_OPERANDS], c % UNIT_OPERANDS, x_q, c, c == 0, c == I_PASSES - 1)
+            nc.scalar.activation(out=blend, in_=acc[:, 0:B], func=ACT.Gelu, bias=bias_in[:, m : m + 1])
+            columns = slice(m * B, (m + 1) * B)
+            nc.vector.tensor_tensor(out=blend, in0=blend, in1=rest[:, columns], op=ALU.add)
+            nc.vector.scalar_tensor_tensor(
+                out=blend, in0=tanh_t[:, columns], scalar=1.0, in1=blend, op0=ALU.add, op1=ALU.mult
             )
-            if e == 1:
-                columns = slice(2 * a * B, 2 * (a + 1) * B)
-                nc.vector.tensor_tensor(out=blends[a][:], in0=blends[a][:], in1=rest[:, columns], op=ALU.add)
-                nc.vector.scalar_tensor_tensor(
-                    out=blends[a][:], in0=tanh_t[:, columns], scalar=1.0, in1=blends[a][:], op0=ALU.add, op1=ALU.mult
-                )
 
         def write_out(a):
             flipped = flip_pool.tile([P, BANK], F32, name="flipped")
@@ -300,18 +326,18 @@ def tile_cfccell_pa_k_kernel(
                     out=result[:].rearrange("b (t p e) -> b t p e", t=BATCH_TILES, e=2)[:, t, :, :],
                     in0=flipped[:].rearrange("b (t e p) -> b t p e", t=BATCH_TILES, e=2)[:, t, :, :],
                     scalar=0.5,
-                    in1=hx_raw[:].rearrange("b (t a p e) -> b t a p e", t=BATCH_TILES, a=4, e=2)[:, t, a, :, :],
+                    in1=hx_raw[:].rearrange("b (t a p e) -> b t a p e", t=BATCH_TILES, a=PAIRS, e=2)[:, t, a, :, :],
                     op0=ALU.mult,
                     op1=ALU.add,
                 )
-            nc.sync.dma_start(
-                out=out.rearrange("(t b) (a f) -> b t a f", b=P, a=4)[:, :, a, :],
-                in_=result[:].rearrange("b (t f) -> b t f", t=BATCH_TILES),
-            )
+                nc.sync.dma_start(
+                    out=out.rearrange("(t b) (a f) -> t b a f", b=P, a=PAIRS)[t, :, a, :],
+                    in_=result[:, t * 2 * P : (t + 1) * 2 * P],
+                )
 
         for m in range(TILES + 2):
             if m < TILES:
-                w_in[m] = [quantise_weights(U_IN + 2 * m), quantise_weights(U_IN + 2 * m + 1)]
+                w_in[m] = weight_pair(U_IN + 2 * m)
             if m >= 3 and m % 2 == 1:
                 write_out((m - 3) // 2)
             if 1 <= m <= TILES:

@@ -40,8 +40,7 @@ AHEAD = RAW_BUFS - 1
 GROUPED_BUFS = 3
 WEIGHT_BUFS = 6
 WORK_BUFS = 2
-FLIP_BANKS = 6
-SUM_BANKS = 2
+BANKS = 8
 
 SCALAR_BANKS = 3
 GELU_UNIT_SCALAR_BANKS = 2
@@ -60,8 +59,7 @@ def tile_cfccell_pa_k_kernel(
         group_pool = ctx.enter_context(tc.tile_pool(name="group", bufs=GROUPED_BUFS))
         weight_pool = ctx.enter_context(tc.tile_pool(name="weight", bufs=WEIGHT_BUFS))
         work = ctx.enter_context(tc.tile_pool(name="work", bufs=WORK_BUFS))
-        flip_pool = ctx.enter_context(tc.psum_pool(name="flip", bufs=FLIP_BANKS))
-        acc_pool = ctx.enter_context(tc.psum_pool(name="acc", bufs=SUM_BANKS))
+        bank_pool = ctx.enter_context(tc.psum_pool(name="bank", bufs=BANKS))
 
         bias_rows = keep.tile([P, 2 * P], BF16, name="bias_rows")
         nc.vector.memset(bias_rows[:], 0.0)
@@ -117,7 +115,7 @@ def tile_cfccell_pa_k_kernel(
         def flip(blocks, grouped, scalar_banks):
             grouped_words = grouped[:].bitcast(F32)
             for b in range(len(blocks) // BANK_FLIPS):
-                flipped = flip_pool.tile([P, BANK], F32, name="flipped")
+                flipped = bank_pool.tile([P, BANK], F32, name="bank")
                 for s in range(BANK_FLIPS):
                     nc.tensor.transpose(flipped[:, s * P : (s + 1) * P], blocks[BANK_FLIPS * b + s], identity[:])
                 source = flipped[:].rearrange("p (j u r) -> p j r u", j=2, u=2)
@@ -173,7 +171,7 @@ def tile_cfccell_pa_k_kernel(
             sums = []
             terms = [(weights, g) for weights in units for g in range(H_PASSES)]
             for pair in range(HALF // 2):
-                acc = acc_pool.tile([P, BANK], F32, name="acc")
+                acc = bank_pool.tile([P, BANK], F32, name="bank")
                 for i in range(2):
                     for n, (weights, g) in enumerate(terms):
                         mx_pass(
@@ -258,7 +256,7 @@ def tile_cfccell_pa_k_kernel(
         quantise(ff1_grouped[:, 0 : BATCH_TILES * H], ff1_q[0][:], ff1_q[1][:])
         w_ff2.append(quantise_weights(w_ff2_grouped))
 
-        flipped_bias = flip_pool.tile([P, BANK], F32, name="flipped")
+        flipped_bias = bank_pool.tile([P, BANK], F32, name="bank")
         nc.tensor.transpose(flipped_bias[:, 0:P], bias_rows[:].bitcast(F32), identity[:])
         bias = keep.tile([P, BIASES * TILES], F32, name="bias")
         nc.vector.tensor_copy(out=bias[:], in_=flipped_bias[:, 0 : BIASES * PAIRS].bitcast(BF16))
@@ -301,7 +299,7 @@ def tile_cfccell_pa_k_kernel(
             if e == 0:
                 blends[a] = work.tile([P, 2 * B], F32, name="blend")
             blend = blends[a][:, e * B : (e + 1) * B]
-            acc = acc_pool.tile([P, BANK], F32, name="acc")
+            acc = bank_pool.tile([P, BANK], F32, name="bank")
             for c in range(I_PASSES):
                 mx_pass(acc[:, 0:B], w_in[m][c // UNIT_OPERANDS], c % UNIT_OPERANDS, x_q, c, c == 0, c == I_PASSES - 1)
             nc.scalar.activation(out=blend, in_=acc[:, 0:B], func=ACT.Gelu, bias=bias_in[:, m : m + 1])
@@ -312,7 +310,7 @@ def tile_cfccell_pa_k_kernel(
             )
 
         def write_out(a):
-            flipped = flip_pool.tile([P, BANK], F32, name="flipped")
+            flipped = bank_pool.tile([P, BANK], F32, name="bank")
             for t in range(BATCH_TILES):
                 for e in range(2):
                     nc.tensor.transpose(

@@ -112,6 +112,16 @@ def tile_cfccell_pa_k_kernel(
         nc.vector.memset(warm[:], 0.0)
         nc.scalar.activation(out=warm[:, 1:2], in_=warm[:, 0:1], func=ACT.Gelu)
 
+        zeros = keep.tile([P, BANK], BF16, name="zeros")
+        nc.vector.memset(zeros[:], 0.0)
+
+        def keep_warm(count):
+            spare = bank_pool.tile([P, BANK], F32, name="bank")
+            for i in range(count):
+                nc.tensor.matmul(spare[:], lhsT=zeros[:, 0:P], rhs=zeros[:], start=True, stop=True)
+
+        keep_warm(6)
+
         def flip(blocks, grouped, scalar_banks):
             grouped_words = grouped[:].bitcast(F32)
             for b in range(len(blocks) // BANK_FLIPS):
@@ -252,6 +262,7 @@ def tile_cfccell_pa_k_kernel(
 
         ff1_grouped = group_pool.tile([P, UNIT], BF16, name="grouped", align_bytes=64)
         flip_activations(ff1_raw[:], H_PASSES, ff1_grouped)
+        keep_warm(2)
         w_ff2_grouped = flip_weights(U_FF2, GELU_UNIT_SCALAR_BANKS)
         quantise(ff1_grouped[:, 0 : BATCH_TILES * H], ff1_q[0][:], ff1_q[1][:])
         w_ff2.append(quantise_weights(w_ff2_grouped))
@@ -271,6 +282,7 @@ def tile_cfccell_pa_k_kernel(
         half_bias_t = keep.tile([P, TILES], F32, name="half_bias_t")
         nc.vector.tensor_scalar_mul(out=half_bias_t[:], in0=bias_sums[:, 0:TILES], scalar1=0.5)
 
+        keep_warm(4)
         w_ff2_grouped = flip_weights(U_FF2 + 1, GELU_UNIT_SCALAR_BANKS)
         flip_activations(hx_raw[:], H_PASSES, hx_grouped)
         w_ff2.append(quantise_weights(w_ff2_grouped))
@@ -290,53 +302,89 @@ def tile_cfccell_pa_k_kernel(
         x_pair(0)
         gate_part(1, w_t1)
         x_pair(2)
+        keep_warm(2)
 
         w_in = {}
         blends = {}
 
-        def input_product(m):
+        def input_gelu(m, acc, start, stop):
             a, e = divmod(m, 2)
-            if e == 0:
+            if a not in blends:
                 blends[a] = work.tile([P, 2 * B], F32, name="blend")
-            blend = blends[a][:, e * B : (e + 1) * B]
+            nc.scalar.activation(
+                out=blends[a][:, e * B + start : e * B + stop], in_=acc[:, start:stop], func=ACT.Gelu,
+                bias=bias_in[:, m : m + 1],
+            )
+
+        def add_rest(m, start, stop):
+            a, e = divmod(m, 2)
+            blend = blends[a][:, e * B + start : e * B + stop]
+            nc.vector.tensor_tensor(out=blend, in0=blend, in1=rest[:, m * B + start : m * B + stop], op=ALU.add)
+
+        def scale_blend(m, start, stop):
+            a, e = divmod(m, 2)
+            blend = blends[a][:, e * B + start : e * B + stop]
+            nc.vector.scalar_tensor_tensor(
+                out=blend, in0=tanh_t[:, m * B + start : m * B + stop], scalar=1.0, in1=blend, op0=ALU.add, op1=ALU.mult
+            )
+
+        def input_passes(m):
             acc = bank_pool.tile([P, BANK], F32, name="bank")
             for c in range(I_PASSES):
                 mx_pass(acc[:, 0:B], w_in[m][c // UNIT_OPERANDS], c % UNIT_OPERANDS, x_q, c, c == 0, c == I_PASSES - 1)
-            nc.scalar.activation(out=blend, in_=acc[:, 0:B], func=ACT.Gelu, bias=bias_in[:, m : m + 1])
-            columns = slice(m * B, (m + 1) * B)
-            nc.vector.tensor_tensor(out=blend, in0=blend, in1=rest[:, columns], op=ALU.add)
+            return acc
+
+        def flip_back(flipped, a, e, t):
+            nc.tensor.transpose(flipped, blends[a][:, e * B + t * P : e * B + (t + 1) * P], identity[:])
+
+        def store(flipped, result, a, t):
             nc.vector.scalar_tensor_tensor(
-                out=blend, in0=tanh_t[:, columns], scalar=1.0, in1=blend, op0=ALU.add, op1=ALU.mult
+                out=result[:].rearrange("b (t p e) -> b t p e", t=BATCH_TILES, e=2)[:, t, :, :],
+                in0=flipped.rearrange("b (e p) -> b p e", e=2),
+                scalar=0.5,
+                in1=hx_raw[:].rearrange("b (t a p e) -> b t a p e", t=BATCH_TILES, a=PAIRS, e=2)[:, t, a, :, :],
+                op0=ALU.mult,
+                op1=ALU.add,
+            )
+            nc.sync.dma_start(
+                out=out.rearrange("(t b) (a f) -> t b a f", b=P, a=PAIRS)[t, :, a, :],
+                in_=result[:, t * 2 * P : (t + 1) * 2 * P],
             )
 
         def write_out(a):
             flipped = bank_pool.tile([P, BANK], F32, name="bank")
             for t in range(BATCH_TILES):
                 for e in range(2):
-                    nc.tensor.transpose(
-                        flipped[:, (2 * t + e) * P : (2 * t + e + 1) * P],
-                        blends[a][:, e * B + t * P : e * B + (t + 1) * P],
-                        identity[:],
-                    )
+                    flip_back(flipped[:, (2 * t + e) * P : (2 * t + e + 1) * P], a, e, t)
             result = work.tile([P, BATCH_TILES * 2 * P], F32, name="result")
             for t in range(BATCH_TILES):
-                nc.vector.scalar_tensor_tensor(
-                    out=result[:].rearrange("b (t p e) -> b t p e", t=BATCH_TILES, e=2)[:, t, :, :],
-                    in0=flipped[:].rearrange("b (t e p) -> b t p e", t=BATCH_TILES, e=2)[:, t, :, :],
-                    scalar=0.5,
-                    in1=hx_raw[:].rearrange("b (t a p e) -> b t a p e", t=BATCH_TILES, a=PAIRS, e=2)[:, t, a, :, :],
-                    op0=ALU.mult,
-                    op1=ALU.add,
-                )
-                nc.sync.dma_start(
-                    out=out.rearrange("(t b) (a f) -> t b a f", b=P, a=PAIRS)[t, :, a, :],
-                    in_=result[:, t * 2 * P : (t + 1) * 2 * P],
-                )
+                store(flipped[:, 2 * t * P : 2 * (t + 1) * P], result, a, t)
 
-        for m in range(TILES + 2):
-            if m < TILES:
-                w_in[m] = weight_pair(U_IN + 2 * m)
+        last, last_pair = TILES - 1, PAIRS - 1
+        for m in range(TILES):
+            w_in[m] = weight_pair(U_IN + 2 * m)
+            if m == 0:
+                keep_warm(2)
             if m >= 3 and m % 2 == 1:
                 write_out((m - 3) // 2)
-            if 1 <= m <= TILES:
-                input_product(m - 1)
+            if m >= 1:
+                acc = input_passes(m - 1)
+                input_gelu(m - 1, acc, 0, B)
+                add_rest(m - 1, 0, B)
+                scale_blend(m - 1, 0, B)
+
+        acc = input_passes(last)
+        batch_tiles = [(t * P, (t + 1) * P) for t in range(BATCH_TILES)]
+        for start, stop in batch_tiles:
+            input_gelu(last, acc, start, stop)
+        banks = [bank_pool.tile([P, BANK], F32, name="bank") for t in range(BATCH_TILES)]
+        for t in range(BATCH_TILES):
+            flip_back(banks[t][:, 0:P], last_pair, 0, t)
+        for start, stop in batch_tiles:
+            add_rest(last, start, stop)
+        for t, (start, stop) in enumerate(batch_tiles):
+            scale_blend(last, start, stop)
+            flip_back(banks[t][:, P : 2 * P], last_pair, 1, t)
+        result = work.tile([P, BATCH_TILES * 2 * P], F32, name="result")
+        for t in range(BATCH_TILES):
+            store(banks[t][:, 0 : 2 * P], result, last_pair, t)

from contextlib import ExitStack

import concourse.mybir as mybir
from concourse.masks import make_identity

F32 = mybir.dt.float32
BF16 = mybir.dt.bfloat16
U32 = mybir.dt.uint32
U8 = mybir.dt.uint8
FP8X4 = mybir.dt.float8_e4m3fn_x4
ACT = mybir.ActivationFunctionType
ALU = mybir.AluOpType

P = 128
B, I, H = 256, 8192, 1024
FLOPS = 2 * B * H * (I + 4 * H)

PACK = 4
K_PASS = P * PACK
WORDS_PASS = K_PASS // 2
H_PASSES = H // K_PASS
I_PASSES = I // K_PASS
BANK = 512
BANK_FLIPS = BANK // P
UNIT = 4096
UNIT_BANKS = UNIT // 2 // BANK
UNIT_WORDS = UNIT // PACK
UNIT_OPERANDS = UNIT // K_PASS
TILES = H // P
PAIRS = TILES // 2
HALF = UNIT_OPERANDS // H_PASSES
assert HALF == PACK
BATCH_TILES = B // P
X_UNITS = B * I // (P * UNIT)
assert X_UNITS == 4
BIASES = 6

RAW_BUFS = 10
AHEAD = RAW_BUFS - 1
GROUPED_BUFS = 3
WEIGHT_BUFS = 6
WORK_BUFS = 2
BANKS = 8

SCALAR_BANKS = 3
GELU_UNIT_SCALAR_BANKS = 2

U_FF2, U_R, U_T, U_X, U_IN = 0, 2, 4, 8, 12


def tile_cfccell_pa_k_kernel(
    tc, ff1, x, hx, W_ff2, b_ff2, W_ta, b_ta, W_tb, b_tb, W_in, b_in, input_b, W_r, r_b, out
):
    nc = tc.nc
    with ExitStack() as ctx:
        ctx.enter_context(tc.manual_schedule())
        keep = ctx.enter_context(tc.tile_pool(name="keep", bufs=1))
        raw_pool = ctx.enter_context(tc.tile_pool(name="raw", bufs=RAW_BUFS))
        group_pool = ctx.enter_context(tc.tile_pool(name="group", bufs=GROUPED_BUFS))
        weight_pool = ctx.enter_context(tc.tile_pool(name="weight", bufs=WEIGHT_BUFS))
        work = ctx.enter_context(tc.tile_pool(name="work", bufs=WORK_BUFS))
        bank_pool = ctx.enter_context(tc.psum_pool(name="bank", bufs=BANKS))

        bias_rows = keep.tile([P, 2 * P], BF16, name="bias_rows")
        nc.vector.memset(bias_rows[:], 0.0)
        for v, vector in enumerate((b_ff2, r_b, b_ta, b_tb, b_in, input_b)):
            nc.scalar.dma_start(
                out=bias_rows[PAIRS * v : PAIRS * (v + 1), :], in_=vector.rearrange("(r c) -> r c", c=2 * P)
            )

        def weight_halves(w):
            rows = w.rearrange("(a p e) k -> p a (e k)", p=P, e=2)
            return [rows[:, 0 : PAIRS // 2, :], rows[:, PAIRS // 2 : PAIRS, :]]

        x_rows = x.rearrange("(t p) k -> p t k", p=P)
        w_in_rows = W_in.rearrange("(a p e) k -> p a e k", p=P, e=2)
        ta_halves, tb_halves = weight_halves(W_ta), weight_halves(W_tb)
        sources = weight_halves(W_ff2) + weight_halves(W_r)
        sources += [ta_halves[0], tb_halves[0], ta_halves[1], tb_halves[1]]
        sources += [x_rows[:, :, q * UNIT // 2 : (q + 1) * UNIT // 2] for q in range(X_UNITS)]
        sources += [
            w_in_rows[:, m // 2, m % 2 : m % 2 + 1, half * UNIT : (half + 1) * UNIT]
            for m in range(TILES)
            for half in range(2)
        ]
        raws = []

        def load_unit(n):
            if n < len(sources):
                raw = raw_pool.tile([P, UNIT], BF16, name="raw")
                nc.sync.dma_start(
                    out=raw[:].rearrange("p (n w) -> p n w", n=sources[n].shape[1]), in_=sources[n]
                )
                raws.append(raw)

        ff1_raw = keep.tile([P, BATCH_TILES * H], BF16, name="ff1_raw")
        hx_raw = keep.tile([P, BATCH_TILES * H], BF16, name="hx_raw")
        nc.sync.dma_start(
            out=ff1_raw[:].rearrange("p (t k) -> p t k", t=BATCH_TILES), in_=ff1.rearrange("(t p) k -> p t k", p=P)
        )
        for n in range(AHEAD):
            if n == U_R:
                nc.sync.dma_start(
                    out=hx_raw[:].rearrange("p (t k) -> p t k", t=BATCH_TILES),
                    in_=hx.rearrange("(t p) k -> p t k", p=P),
                )
            load_unit(n)

        identity = keep.tile([P, P], F32, name="identity")
        make_identity(nc, identity[:])
        warm = keep.tile([P, 2], F32, name="warm")
        nc.vector.memset(warm[:], 0.0)
        nc.scalar.activation(out=warm[:, 1:2], in_=warm[:, 0:1], func=ACT.Gelu)

        zeros = keep.tile([P, BANK], BF16, name="zeros")
        nc.vector.memset(zeros[:], 0.0)

        def keep_warm(count):
            spare = bank_pool.tile([P, BANK], F32, name="bank")
            for i in range(count):
                nc.tensor.matmul(spare[:], lhsT=zeros[:, 0:P], rhs=zeros[:], start=True, stop=True)

        keep_warm(6)

        def flip(blocks, grouped, scalar_banks):
            grouped_words = grouped[:].bitcast(F32)
            for b in range(len(blocks) // BANK_FLIPS):
                flipped = bank_pool.tile([P, BANK], F32, name="bank")
                for s in range(BANK_FLIPS):
                    nc.tensor.transpose(flipped[:, s * P : (s + 1) * P], blocks[BANK_FLIPS * b + s], identity[:])
                source = flipped[:].rearrange("p (j u r) -> p j r u", j=2, u=2)
                target = grouped_words[:, b * BANK : (b + 1) * BANK].rearrange("p (j r u) -> p j r u", j=2, u=2)
                if b % UNIT_BANKS < scalar_banks:
                    nc.scalar.copy(out=target, in_=source)
                else:
                    nc.vector.tensor_copy(out=target, in_=source)

        def quantise(grouped, codes, scales):
            nc.vector.quantize_mx(out=codes.bitcast(FP8X4), scales=scales, in_=grouped)

        def flip_activations(raw, passes, grouped):
            words = raw.bitcast(F32)
            blocks = [
                words[:, (t * passes + c) * WORDS_PASS + u * P : (t * passes + c) * WORDS_PASS + (u + 1) * P]
                for c in range(passes)
                for t in range(BATCH_TILES)
                for u in range(2)
            ]
            flip(blocks, grouped, SCALAR_BANKS)

        def flip_weights(n, scalar_banks):
            load_unit(n + AHEAD)
            words = raws[n][:].bitcast(F32)
            grouped = group_pool.tile([P, UNIT], BF16, name="grouped", align_bytes=64)
            flip([words[:, s * P : (s + 1) * P] for s in range(UNIT // 2 // P)], grouped, scalar_banks)
            return grouped

        def quantise_weights(grouped):
            codes = weight_pool.tile([P, UNIT_WORDS], U32, name="w_codes", align_bytes=64)
            scales = weight_pool.tile([P, UNIT_WORDS], U8, name="w_scales", align_bytes=64)
            quantise(grouped[:], codes[:], scales[:])
            return codes, scales

        def weight_pair(n, scalar_banks=SCALAR_BANKS):
            first = flip_weights(n, scalar_banks)
            second = flip_weights(n + 1, scalar_banks)
            return [quantise_weights(first), quantise_weights(second)]

        def mx_pass(acc, weights, j, moving, c, start, stop):
            nc.tensor.matmul_mx(
                out=acc,
                lhsT=weights[0][:, j * P : (j + 1) * P].bitcast(FP8X4),
                lhsT_scale=weights[1][:, j * P : (j + 1) * P],
                rhs=moving[0][:, c * B : (c + 1) * B].bitcast(FP8X4),
                rhs_scale=moving[1][:, c * B : (c + 1) * B],
                start=start,
                stop=stop,
            )

        def small_products(units, moving):
            sums = []
            terms = [(weights, g) for weights in units for g in range(H_PASSES)]
            for pair in range(HALF // 2):
                acc = bank_pool.tile([P, BANK], F32, name="bank")
                for i in range(2):
                    for n, (weights, g) in enumerate(terms):
                        mx_pass(
                            acc[:, i * B : (i + 1) * B], weights, H_PASSES * (2 * pair + i) + g, moving, g,
                            n == 0, n == len(terms) - 1,
                        )
                    sums.append(acc[:, i * B : (i + 1) * B])
            return sums

        def activation_tiles(name, passes):
            codes = keep.tile([P, passes * B], U32, name=name + "_codes", align_bytes=64)
            scales = keep.tile([P, passes * B], U8, name=name + "_scales", align_bytes=64)
            return codes, scales

        ff1_q = activation_tiles("ff1", H_PASSES)
        ff2_q = activation_tiles("ff2", H_PASSES)
        hx_q = activation_tiles("hx", H_PASSES)
        x_q = activation_tiles("x", I_PASSES)

        w_ff2 = []
        ff2_t = {}

        def hidden_products(g):
            ff2_t[g] = work.tile([P, HALF * B], BF16, name="ff2_t")
            for i, acc in enumerate(small_products([w_ff2[g]], ff1_q)):
                nc.scalar.activation(
                    out=ff2_t[g][:, i * B : (i + 1) * B], in_=acc, func=ACT.Gelu,
                    bias=bias_ff2[:, HALF * g + i : HALF * g + i + 1],
                )

        def hidden_quantise(g):
            grouped = group_pool.tile([P, UNIT], BF16, name="grouped", align_bytes=64)
            nc.vector.tensor_copy(
                out=grouped[:, 0 : PACK * B].rearrange("p (b i) -> p b i", i=PACK),
                in_=ff2_t[g][:].rearrange("p (i b) -> p b i", i=HALF),
            )
            quantise(grouped[:, 0 : PACK * B], ff2_q[0][:, g * B : (g + 1) * B], ff2_q[1][:, g * B : (g + 1) * B])

        tanh_t = keep.tile([P, TILES * B], F32, name="tanh_t")

        def gate_part(half, units):
            for i, acc in enumerate(small_products(units, ff2_q)):
                m = HALF * half + i
                nc.scalar.activation(
                    out=tanh_t[:, m * B : (m + 1) * B], in_=acc, func=ACT.Tanh, bias=half_bias_t[:, m : m + 1], scale=0.5
                )

        hx_grouped = keep.tile([P, TILES * B], BF16, name="hx_grouped", align_bytes=64)
        rest = keep.tile([P, TILES * B], F32, name="rest")
        gelu_r = {}

        def recurrent_products(half, weights):
            gelu_r[half] = work.tile([P, HALF * B], F32, name="gelu_r")
            for i, acc in enumerate(small_products([weights], hx_q)):
                nc.scalar.activation(
                    out=gelu_r[half][:, i * B : (i + 1) * B], in_=acc, func=ACT.Gelu,
                    bias=bias_r[:, HALF * half + i : HALF * half + i + 1],
                )

        def recurrent_rest(half):
            columns = slice(HALF * half * B, HALF * (half + 1) * B)
            nc.vector.tensor_tensor(
                out=rest[:, columns].rearrange("p (i b) -> p i b", i=HALF),
                in0=gelu_r[half][:].rearrange("p (i b) -> p i b", i=HALF),
                in1=hx_grouped[:, columns].rearrange("p (b i) -> p i b", i=PACK),
                op=ALU.subtract,
            )

        def x_pair(q):
            grouped = []
            for n in (q, q + 1):
                load_unit(U_X + n + AHEAD)
                grouped.append(group_pool.tile([P, UNIT], BF16, name="grouped", align_bytes=64))
                flip_activations(raws[U_X + n][:], UNIT // 2 // K_PASS, grouped[-1])
            for i, n in enumerate((q, q + 1)):
                columns = slice(n * UNIT_WORDS, (n + 1) * UNIT_WORDS)
                quantise(grouped[i][:], x_q[0][:, columns], x_q[1][:, columns])

        ff1_grouped = group_pool.tile([P, UNIT], BF16, name="grouped", align_bytes=64)
        flip_activations(ff1_raw[:], H_PASSES, ff1_grouped)
        keep_warm(2)
        w_ff2_grouped = flip_weights(U_FF2, GELU_UNIT_SCALAR_BANKS)
        quantise(ff1_grouped[:, 0 : BATCH_TILES * H], ff1_q[0][:], ff1_q[1][:])
        w_ff2.append(quantise_weights(w_ff2_grouped))

        flipped_bias = bank_pool.tile([P, BANK], F32, name="bank")
        nc.tensor.transpose(flipped_bias[:, 0:P], bias_rows[:].bitcast(F32), identity[:])
        bias = keep.tile([P, BIASES * TILES], F32, name="bias")
        nc.vector.tensor_copy(out=bias[:], in_=flipped_bias[:, 0 : BIASES * PAIRS].bitcast(BF16))
        bias_ff2, bias_r = bias[:, 0:TILES], bias[:, TILES : 2 * TILES]
        bias_sums = keep.tile([P, 2 * TILES], F32, name="bias_sums")
        addends = bias[:, 2 * TILES : BIASES * TILES].rearrange("p (s w m) -> p s w m", s=2, w=2)
        nc.vector.tensor_tensor(
            out=bias_sums[:].rearrange("p (s m) -> p s m", s=2), in0=addends[:, :, 0, :], in1=addends[:, :, 1, :],
            op=ALU.add,
        )
        bias_in = bias_sums[:, TILES : 2 * TILES]
        half_bias_t = keep.tile([P, TILES], F32, name="half_bias_t")
        nc.vector.tensor_scalar_mul(out=half_bias_t[:], in0=bias_sums[:, 0:TILES], scalar1=0.5)

        keep_warm(4)
        w_ff2_grouped = flip_weights(U_FF2 + 1, GELU_UNIT_SCALAR_BANKS)
        flip_activations(hx_raw[:], H_PASSES, hx_grouped)
        w_ff2.append(quantise_weights(w_ff2_grouped))
        quantise(hx_grouped[:], hx_q[0][:], hx_q[1][:])
        hidden_products(0)
        w_r = weight_pair(U_R, GELU_UNIT_SCALAR_BANKS)
        hidden_products(1)
        hidden_quantise(0)
        w_t0 = weight_pair(U_T)
        hidden_quantise(1)
        recurrent_products(0, w_r[0])
        recurrent_products(1, w_r[1])
        w_t1 = weight_pair(U_T + 2)
        recurrent_rest(0)
        recurrent_rest(1)
        gate_part(0, w_t0)
        x_pair(0)
        gate_part(1, w_t1)
        x_pair(2)
        keep_warm(2)

        w_in = {}
        blends = {}

        def input_gelu(m, acc, start, stop):
            a, e = divmod(m, 2)
            if a not in blends:
                blends[a] = work.tile([P, 2 * B], F32, name="blend")
            nc.scalar.activation(
                out=blends[a][:, e * B + start : e * B + stop], in_=acc[:, start:stop], func=ACT.Gelu,
                bias=bias_in[:, m : m + 1],
            )

        def add_rest(m, start, stop):
            a, e = divmod(m, 2)
            blend = blends[a][:, e * B + start : e * B + stop]
            nc.vector.tensor_tensor(out=blend, in0=blend, in1=rest[:, m * B + start : m * B + stop], op=ALU.add)

        def scale_blend(m, start, stop):
            a, e = divmod(m, 2)
            blend = blends[a][:, e * B + start : e * B + stop]
            nc.vector.scalar_tensor_tensor(
                out=blend, in0=tanh_t[:, m * B + start : m * B + stop], scalar=1.0, in1=blend, op0=ALU.add, op1=ALU.mult
            )

        def input_passes(m):
            acc = bank_pool.tile([P, BANK], F32, name="bank")
            for c in range(I_PASSES):
                mx_pass(acc[:, 0:B], w_in[m][c // UNIT_OPERANDS], c % UNIT_OPERANDS, x_q, c, c == 0, c == I_PASSES - 1)
            return acc

        def flip_back(flipped, a, e, t):
            nc.tensor.transpose(flipped, blends[a][:, e * B + t * P : e * B + (t + 1) * P], identity[:])

        def store(flipped, result, a, t):
            nc.vector.scalar_tensor_tensor(
                out=result[:].rearrange("b (t p e) -> b t p e", t=BATCH_TILES, e=2)[:, t, :, :],
                in0=flipped.rearrange("b (e p) -> b p e", e=2),
                scalar=0.5,
                in1=hx_raw[:].rearrange("b (t a p e) -> b t a p e", t=BATCH_TILES, a=PAIRS, e=2)[:, t, a, :, :],
                op0=ALU.mult,
                op1=ALU.add,
            )
            nc.sync.dma_start(
                out=out.rearrange("(t b) (a f) -> t b a f", b=P, a=PAIRS)[t, :, a, :],
                in_=result[:, t * 2 * P : (t + 1) * 2 * P],
            )

        def write_out(a):
            flipped = bank_pool.tile([P, BANK], F32, name="bank")
            for t in range(BATCH_TILES):
                for e in range(2):
                    flip_back(flipped[:, (2 * t + e) * P : (2 * t + e + 1) * P], a, e, t)
            result = work.tile([P, BATCH_TILES * 2 * P], F32, name="result")
            for t in range(BATCH_TILES):
                store(flipped[:, 2 * t * P : 2 * (t + 1) * P], result, a, t)

        last, last_pair = TILES - 1, PAIRS - 1
        for m in range(TILES):
            w_in[m] = weight_pair(U_IN + 2 * m)
            if m == 0:
                keep_warm(2)
            if m >= 3 and m % 2 == 1:
                write_out((m - 3) // 2)
            if m >= 1:
                acc = input_passes(m - 1)
                input_gelu(m - 1, acc, 0, B)
                add_rest(m - 1, 0, B)
                scale_blend(m - 1, 0, B)

        acc = input_passes(last)
        batch_tiles = [(t * P, (t + 1) * P) for t in range(BATCH_TILES)]
        for start, stop in batch_tiles:
            input_gelu(last, acc, start, stop)
        banks = [bank_pool.tile([P, BANK], F32, name="bank") for t in range(BATCH_TILES)]
        for t in range(BATCH_TILES):
            flip_back(banks[t][:, 0:P], last_pair, 0, t)
        for start, stop in batch_tiles:
            add_rest(last, start, stop)
        for t, (start, stop) in enumerate(batch_tiles):
            scale_blend(last, start, stop)
            flip_back(banks[t][:, P : 2 * P], last_pair, 1, t)
        result = work.tile([P, BATCH_TILES * 2 * P], F32, name="result")
        for t in range(BATCH_TILES):
            store(banks[t][:, 0 : 2 * P], result, last_pair, t)
